import numpy as np
import ml_dtypes


def mxq(x, axis, fmt="e4m3"):
    dtype, down = {"e4m3": (ml_dtypes.float8_e4m3fn, 7), "e5m2": (ml_dtypes.float8_e5m2, 14)}[fmt]
    v = np.moveaxis(np.asarray(x, np.float32).astype(ml_dtypes.bfloat16).astype(np.float64), axis, -1)
    blocks = v.reshape(v.shape[:-1] + (-1, 32))
    amax = np.abs(blocks).max(-1, keepdims=True)
    byte = np.maximum(np.where(amax > 0, np.frexp(amax)[1] - 1 + 127, 0) - down, 1)
    scale = np.exp2(byte - 127.0)
    codes = (blocks / scale).astype(np.float32).astype(dtype).astype(np.float64)
    return np.moveaxis((codes * scale).reshape(v.shape), -1, axis)


WIDE = False


def mx_kscale(k):
    if not WIDE:
        return np.ones(k)
    levels = np.array([10, -10, 5, -5, 0])
    a = np.random.permutation(np.resize(levels, k // 512 * 4)).reshape(k // 512, 4)
    idx = np.arange(k)
    return np.exp2(a[idx // 512, idx % 128 // 32])


BF16 = ml_dtypes.bfloat16


def bf(x):
    return np.asarray(x, np.float32).astype(BF16)


def f64(x):
    return np.asarray(x).astype(np.float64)


B, N, C, C4, FX, FY = 512, 8, 512, 128, 10, 13
EPS_L1 = 1e-9


def setup_inputs():
    s = mx_kscale(C)
    qk = np.sqrt(2.5 / np.sqrt(C4))
    return {"xq": bf(np.random.standard_normal((N, B, C4)) * qk),
            "yk": bf(np.random.standard_normal((N, B, C4)) * qk),
            "y_feat": bf(np.random.standard_normal((B, N, C)) * s),
            "x_feat": bf(np.random.standard_normal((B, N, C))),
            "W_v": bf(np.random.standard_normal((C, C)) / np.sqrt(C) / s[None, :]),
            "b_v": bf(np.random.standard_normal(C) * 0.3)}


def reference(xq, yk, y_feat, x_feat, W_v, b_v):
    yv = ((mxq(f64(y_feat), 2, "e4m3") @ mxq(f64(W_v), 1, "e4m3").T) + f64(b_v)).transpose(1, 0, 2)
    energy = f64(xq) @ f64(yk).transpose(0, 2, 1)
    p = np.exp(energy - energy.max(axis=-1, keepdims=True))
    attn = p / p.sum(axis=-1, keepdims=True)
    attn = attn / (EPS_L1 + attn.sum(axis=1, keepdims=True))
    yr = (mxq(attn, 2, "e4m3") @ mxq(yv, 1, "e4m3")).transpose(1, 0, 2)
    return f64(x_feat) - yr

@@ -1,0 +1,286 @@
+from contextlib import ExitStack
+
+import concourse.mybir as mybir
+from concourse.masks import make_identity
+
+F32 = mybir.dt.float32
+BF16 = mybir.dt.bfloat16
+U32 = mybir.dt.uint32
+U8 = mybir.dt.uint8
+FP8X4 = mybir.dt.float8_e4m3fn_x4
+ALU = mybir.AluOpType
+ACT = mybir.ActivationFunctionType
+
+P = 128
+PACK = 4
+POINTS = 8
+ENTRIES = 512
+CHANNELS = 512
+QK = 128
+EPS_L1 = 1e-9
+
+FLOPS = 2 * POINTS * ENTRIES * (CHANNELS * CHANNELS + ENTRIES * QK + ENTRIES * CHANNELS)
+
+
+PROJECTIONS_LEAD = 4
+VALUES_DELAY = 5
+FLIP_DELAY = 4
+COLUMNS_DELAY = 8
+QUANTISE_DELAY = 9
+OUTPUT_DELAY = 10
+QUARTERS = POINTS * PACK
+
+
+def tile_interral_pa_kernel(tc, xq, yk, y_feat, x_feat, W_v, b_v, out):
+    nc = tc.nc
+    with ExitStack() as ctx:
+        resident = ctx.enter_context(tc.tile_pool(name="resident", bufs=1))
+        proj = ctx.enter_context(tc.tile_pool(name="proj", bufs=3))
+        grouped_pool = ctx.enter_context(tc.tile_pool(name="grouped", bufs=2))
+        mx_pool = ctx.enter_context(tc.tile_pool(name="mx", bufs=3))
+        values_pool = ctx.enter_context(tc.tile_pool(name="values", bufs=4))
+        soft = ctx.enter_context(tc.tile_pool(name="soft", bufs=3))
+        stats = ctx.enter_context(tc.tile_pool(name="stats", bufs=4))
+        result_pool = ctx.enter_context(tc.tile_pool(name="result", bufs=4))
+        psum_flip = ctx.enter_context(tc.psum_pool(name="psum_flip", bufs=2))
+        psum_energy = ctx.enter_context(tc.psum_pool(name="psum_energy", bufs=2))
+        psum_prob = ctx.enter_context(tc.psum_pool(name="psum_prob", bufs=2))
+        psum_mx = ctx.enter_context(tc.psum_pool(name="psum_mx", bufs=2))
+
+        xq_rows = xq.rearrange("n (p g) d -> n p g d", g=PACK)
+        yk_rows = yk.rearrange("n (p g) d -> n p g d", g=PACK)
+        y_rows = y_feat.rearrange("(p g) n k -> n p g k", g=PACK)
+        x_rows = x_feat.rearrange("(p g) n c -> n p g c", g=PACK)
+        out_rows = out.rearrange("(p g) n c -> n g p c", g=PACK)
+
+        xq_sb, yk_sb, y_sb, x_sb = [], [], [], []
+        w_sb = resident.tile([P, PACK, CHANNELS], BF16)
+        bias_sb = resident.tile([P, CHANNELS], BF16)
+        for n in range(POINTS):
+            xq_sb.append(resident.tile([P, PACK, QK], BF16, name="xq%d" % n))
+            yk_sb.append(resident.tile([P, PACK, QK], BF16, name="yk%d" % n))
+            y_sb.append(resident.tile([P, PACK, CHANNELS], BF16, name="y%d" % n))
+            x_sb.append(resident.tile([P, PACK, CHANNELS], BF16, name="x%d" % n))
+            nc.sync.dma_start(out=xq_sb[n][:], in_=xq_rows[n])
+            nc.sync.dma_start(out=yk_sb[n][:], in_=yk_rows[n])
+            if n == 0:
+                nc.sync.dma_start(out=w_sb[:], in_=W_v.rearrange("(i p) k -> p i k", p=P))
+            nc.sync.dma_start(out=y_sb[n][:], in_=y_rows[n])
+            if n == 0:
+                nc.sync.dma_start(out=bias_sb[:], in_=b_v.partition_broadcast(P))
+            else:
+                nc.sync.dma_start(out=x_sb[n - 1][:], in_=x_rows[n - 1])
+        nc.sync.dma_start(out=x_sb[POINTS - 1][:], in_=x_rows[POINTS - 1])
+
+        ident_f32 = resident.tile([P, P], F32)
+        make_identity(nc, ident_f32[:])
+        ident_bf16 = resident.tile([P, P], BF16)
+        make_identity(nc, ident_bf16[:])
+
+        y_grouped, y_codes, y_scales = {}, {}, {}
+        xq_t, yk_t = {}, {}
+        neg_max, row_sum, row_inv, prob = {}, {}, {}, {}
+        yv_grouped, yv_codes, yv_scales = {}, {}, {}
+        col_sum, col_inv, prob_t = {}, {}, {}
+        attn_grouped, attn_codes, attn_scales = {}, {}, {}
+
+        def quantise(codes, scales, grouped, first, count):
+            cols = slice(first, first + count)
+            nc.vector.quantize_mx(
+                out=codes[:, cols].bitcast(FP8X4),
+                scales=scales[:, cols],
+                in_=grouped[:, cols, :].rearrange("q r t -> q (r t)"),
+            )
+
+        def channels_to_partitions(rows_sb, grouped, pair):
+            words = rows_sb[:].bitcast(F32)
+            grouped_words = grouped[:].bitcast(F32).rearrange("q (g r) u -> q g r u", g=PACK)
+            flipped = psum_flip.tile([P, 2, 2, P], F32, tag="flip")
+            for g in range(2):
+                for u in range(2):
+                    nc.tensor.transpose(
+                        flipped[:, g, u, :], words[:, 2 * pair + g, u * P : (u + 1) * P], ident_f32[:]
+                    )
+            nc.scalar.copy(
+                out=grouped_words[:, 2 * pair : 2 * pair + 2],
+                in_=flipped[:].rearrange("q g u r -> q g r u"),
+            )
+
+        def projection_to_partitions(rows_sb, columns):
+            flipped = psum_flip.tile([P, PACK, P], BF16, tag="flip")
+            for g in range(PACK):
+                nc.tensor.transpose(flipped[:, g, :], rows_sb[:, g, :], ident_bf16[:])
+            nc.scalar.copy(out=columns[:], in_=flipped[:].rearrange("d g r -> d (g r)"))
+
+        def prepare_projections(n, j):
+            if j == 0:
+                xq_t[n] = proj.tile([P, ENTRIES], BF16, name="xq_t")
+                projection_to_partitions(xq_sb[n], xq_t[n])
+            elif j == 1:
+                yk_t[n] = proj.tile([P, ENTRIES], BF16, name="yk_t")
+                projection_to_partitions(yk_sb[n], yk_t[n])
+
+        def prepare_features(n, j):
+            if j == 2:
+                y_grouped[n] = grouped_pool.tile([P, ENTRIES, PACK], BF16, name="y_grouped", align_bytes=64)
+                y_codes[n] = mx_pool.tile([P, ENTRIES], U32, name="y_codes", align_bytes=64)
+                y_scales[n] = mx_pool.tile([P, ENTRIES], U8, name="y_scales", align_bytes=64)
+            if j >= 2:
+                channels_to_partitions(y_sb[n], y_grouped[n], j - 2)
+
+        def quantise_features(n, j):
+            if j >= 2:
+                quantise(y_codes[n], y_scales[n], y_grouped[n], 2 * (j - 2) * P, 2 * P)
+
+        def prepare_weights(n, j):
+            if j < 2:
+                channels_to_partitions(w_sb, w_grouped, j)
+
+        def quantise_weights(n, j):
+            if j < 2:
+                quantise(w_codes, w_scales, w_grouped, 2 * j * P, 2 * P)
+
+        def energy_softmax(n, j):
+            if j == 0:
+                neg_max[n] = stats.tile([P, PACK], F32, name="neg_max")
+                row_sum[n] = stats.tile([P, PACK], F32, name="row_sum")
+                row_inv[n] = stats.tile([P, PACK], F32, name="row_inv")
+                prob[n] = soft.tile([P, PACK, ENTRIES], F32, name="prob")
+            energy = psum_energy.tile([P, ENTRIES], F32)
+            nc.tensor.matmul(
+                out=energy[:], lhsT=xq_t[n][:, j * P : (j + 1) * P], rhs=yk_t[n][:], start=True, stop=True
+            )
+            nc.vector.tensor_reduce(
+                out=neg_max[n][:, j : j + 1], in_=energy[:], axis=mybir.AxisListType.X, op=ALU.max, negate=True
+            )
+            nc.scalar.activation(
+                out=prob[n][:, j, :],
+                in_=energy[:],
+                func=ACT.Exp,
+                bias=neg_max[n][:, j : j + 1],
+                scale=1.0,
+                accum_out=row_sum[n][:, j : j + 1],
+            )
+
+        def invert_row_sums(n, j):
+            nc.vector.reciprocal(out=row_inv[n][:, j : j + 1], in_=row_sum[n][:, j : j + 1])
+
+        def scale_rows(n, j):
+            if j % 2 == 0:
+                nc.scalar.activation(
+                    out=prob[n][:, j, :], in_=prob[n][:, j, :], func=ACT.Copy, scale=row_inv[n][:, j : j + 1]
+                )
+            else:
+                nc.gpsimd.tensor_scalar(
+                    out=prob[n][:, j, :],
+                    in0=prob[n][:, j, :],
+                    scalar1=row_inv[n][:, j : j + 1],
+                    scalar2=0.0,
+                    op0=ALU.mult,
+                    op1=ALU.add,
+                )
+
+        def project_values(n, c):
+            if c == 0:
+                yv_grouped[n] = grouped_pool.tile([P, CHANNELS, PACK], BF16, name="yv_grouped", align_bytes=64)
+                yv_codes[n] = values_pool.tile([P, CHANNELS], U32, name="yv_codes", align_bytes=64)
+                yv_scales[n] = values_pool.tile([P, CHANNELS], U8, name="yv_scales", align_bytes=64)
+            cols = slice(c * P, (c + 1) * P)
+            yv_acc = psum_mx.tile([P, PACK, P], F32, tag="acc")
+            for t in range(PACK):
+                keys = slice(t * P, (t + 1) * P)
+                nc.tensor.matmul_mx(
+                    out=yv_acc[:, t, :],
+                    lhsT=y_codes[n][:, keys].bitcast(FP8X4),
+                    lhsT_scale=y_scales[n][:, keys],
+                    rhs=w_codes[:, cols].bitcast(FP8X4),
+                    rhs_scale=w_scales[:, cols],
+                    start=True,
+                    stop=True,
+                )
+            nc.vector.tensor_tensor(
+                out=yv_grouped[n][:, cols, :],
+                in0=yv_acc[:].rearrange("p t c -> p c t"),
+                in1=bias_sb[:, cols].unsqueeze(2).to_broadcast([P, P, PACK]),
+                op=ALU.add,
+            )
+
+        def quantise_values(n, c):
+            quantise(yv_codes[n], yv_scales[n], yv_grouped[n], c * P, P)
+
+        def flip_probabilities(n, t):
+            if t == 0:
+                col_sum[n] = stats.tile([P, PACK], F32, name="col_sum")
+                col_inv[n] = stats.tile([P, PACK], F32, name="col_inv")
+                prob_t[n] = soft.tile([P, PACK, ENTRIES], F32, name="prob_t")
+            flipped_prob = psum_prob.tile([P, ENTRIES], F32)
+            for j in range(PACK):
+                nc.tensor.transpose(
+                    flipped_prob[:, j * P : (j + 1) * P], prob[n][:, j, t * P : (t + 1) * P], ident_f32[:]
+                )
+            nc.scalar.activation(
+                out=prob_t[n][:, t, :], in_=flipped_prob[:], func=ACT.Copy, accum_out=col_sum[n][:, t : t + 1]
+            )
+
+        def invert_column_sums(n, j):
+            if j == 0:
+                nc.vector.tensor_scalar_add(out=col_inv[n][:], in0=col_sum[n][:], scalar1=EPS_L1)
+                nc.vector.reciprocal(out=col_inv[n][:], in_=col_inv[n][:])
+
+        def scale_columns(n, j):
+            if j == 0:
+                attn_grouped[n] = grouped_pool.tile([P, ENTRIES, PACK], BF16, name="attn_grouped", align_bytes=64)
+                attn_codes[n] = mx_pool.tile([P, ENTRIES], U32, name="attn_codes", align_bytes=64)
+                attn_scales[n] = mx_pool.tile([P, ENTRIES], U8, name="attn_scales", align_bytes=64)
+            queries = slice(j * P, (j + 1) * P)
+            nc.gpsimd.tensor_tensor(
+                out=attn_grouped[n][:, queries, :],
+                in0=prob_t[n][:, :, queries].rearrange("p t b -> p b t"),
+                in1=col_inv[n][:].unsqueeze(1).to_broadcast([P, P, PACK]),
+                op=ALU.mult,
+            )
+
+        def quantise_attention(n, j):
+            quantise(attn_codes[n], attn_scales[n], attn_grouped[n], j * P, P)
+
+        def subtract_attended(n, j):
+            queries = slice(j * P, (j + 1) * P)
+            yr_acc = psum_mx.tile([P, CHANNELS], F32, tag="acc")
+            nc.tensor.matmul_mx(
+                out=yr_acc[:],
+                lhsT=attn_codes[n][:, queries].bitcast(FP8X4),
+                lhsT_scale=attn_scales[n][:, queries],
+                rhs=yv_codes[n][:].bitcast(FP8X4),
+                rhs_scale=yv_scales[n][:],
+                start=True,
+                stop=True,
+            )
+            result = result_pool.tile([P, CHANNELS], F32)
+            nc.vector.tensor_tensor(out=result[:], in0=x_sb[n][:, j, :], in1=yr_acc[:], op=ALU.subtract)
+            nc.sync.dma_start(out=out_rows[n, j], in_=result[:])
+
+        def run(stage, index, count=QUARTERS):
+            if 0 <= index < count:
+                stage(index // PACK, index % PACK)
+
+        w_grouped = resident.tile([P, CHANNELS, PACK], BF16, align_bytes=64)
+        w_codes = resident.tile([P, CHANNELS], U32, align_bytes=64)
+        w_scales = resident.tile([P, CHANNELS], U8, align_bytes=64)
+
+        with tc.manual_schedule():
+            for tick in range(-PROJECTIONS_LEAD, QUARTERS + OUTPUT_DELAY):
+                run(scale_rows, tick - 1)
+                run(energy_softmax, tick)
+                run(invert_column_sums, tick - COLUMNS_DELAY)
+                run(project_values, tick - VALUES_DELAY)
+                run(quantise_attention, tick - QUANTISE_DELAY)
+                run(subtract_attended, tick - OUTPUT_DELAY)
+                run(scale_columns, tick - COLUMNS_DELAY)
+                run(quantise_values, tick - VALUES_DELAY - 1)
+                run(quantise_features, tick - 1)
+                run(quantise_weights, tick - 1, PACK)
+                run(flip_probabilities, tick - FLIP_DELAY)
+                run(prepare_projections, tick + PROJECTIONS_LEAD)
+                run(prepare_features, tick)
+                run(prepare_weights, tick, PACK)
+                run(invert_row_sums, tick)

@@ -166,19 +166,9 @@ def tile_interral_pa_kernel(tc, xq, yk, y_feat, x_feat, W_v, b_v, out):
             nc.vector.reciprocal(out=row_inv[n][:, j : j + 1], in_=row_sum[n][:, j : j + 1])
 
         def scale_rows(n, j):
-            if j % 2 == 0:
-                nc.scalar.activation(
-                    out=prob[n][:, j, :], in_=prob[n][:, j, :], func=ACT.Copy, scale=row_inv[n][:, j : j + 1]
-                )
-            else:
-                nc.gpsimd.tensor_scalar(
-                    out=prob[n][:, j, :],
-                    in0=prob[n][:, j, :],
-                    scalar1=row_inv[n][:, j : j + 1],
-                    scalar2=0.0,
-                    op0=ALU.mult,
-                    op1=ALU.add,
-                )
+            nc.scalar.activation(
+                out=prob[n][:, j, :], in_=prob[n][:, j, :], func=ACT.Copy, scale=row_inv[n][:, j : j + 1]
+            )
 
         def project_values(n, c):
             if c == 0:
@@ -233,7 +223,7 @@ def tile_interral_pa_kernel(tc, xq, yk, y_feat, x_feat, W_v, b_v, out):
                 attn_codes[n] = mx_pool.tile([P, ENTRIES], U32, name="attn_codes", align_bytes=64)
                 attn_scales[n] = mx_pool.tile([P, ENTRIES], U8, name="attn_scales", align_bytes=64)
             queries = slice(j * P, (j + 1) * P)
-            nc.gpsimd.tensor_tensor(
+            nc.vector.tensor_tensor(
                 out=attn_grouped[n][:, queries, :],
                 in0=prob_t[n][:, :, queries].rearrange("p t b -> p b t"),
                 in1=col_inv[n][:].unsqueeze(1).to_broadcast([P, P, PACK]),

@@ -26,8 +26,7 @@ PROJECTIONS_LEAD = 4
 VALUES_DELAY = 5
 FLIP_DELAY = 4
 COLUMNS_DELAY = 8
-QUANTISE_DELAY = 9
-OUTPUT_DELAY = 10
+OUTPUT_DELAY = 12
 QUARTERS = POINTS * PACK
 
 
@@ -37,6 +36,7 @@ def tile_interral_pa_kernel(tc, xq, yk, y_feat, x_feat, W_v, b_v, out):
         resident = ctx.enter_context(tc.tile_pool(name="resident", bufs=1))
         proj = ctx.enter_context(tc.tile_pool(name="proj", bufs=3))
         grouped_pool = ctx.enter_context(tc.tile_pool(name="grouped", bufs=2))
+        attn_pool = ctx.enter_context(tc.tile_pool(name="attn", bufs=1))
         mx_pool = ctx.enter_context(tc.tile_pool(name="mx", bufs=3))
         values_pool = ctx.enter_context(tc.tile_pool(name="values", bufs=4))
         soft = ctx.enter_context(tc.tile_pool(name="soft", bufs=3))
@@ -129,16 +129,16 @@ def tile_interral_pa_kernel(tc, xq, yk, y_feat, x_feat, W_v, b_v, out):
                 channels_to_partitions(y_sb[n], y_grouped[n], j - 2)
 
         def quantise_features(n, j):
-            if j >= 2:
-                quantise(y_codes[n], y_scales[n], y_grouped[n], 2 * (j - 2) * P, 2 * P)
+            if j == 0:
+                quantise(y_codes[n], y_scales[n], y_grouped[n], 0, ENTRIES)
 
         def prepare_weights(n, j):
             if j < 2:
                 channels_to_partitions(w_sb, w_grouped, j)
 
         def quantise_weights(n, j):
-            if j < 2:
-                quantise(w_codes, w_scales, w_grouped, 2 * j * P, 2 * P)
+            if j == 0:
+                quantise(w_codes, w_scales, w_grouped, 0, CHANNELS)
 
         def energy_softmax(n, j):
             if j == 0:
@@ -195,8 +195,9 @@ def tile_interral_pa_kernel(tc, xq, yk, y_feat, x_feat, W_v, b_v, out):
                 op=ALU.add,
             )
 
-        def quantise_values(n, c):
-            quantise(yv_codes[n], yv_scales[n], yv_grouped[n], c * P, P)
+        def quantise_values(n, j):
+            if j == 0:
+                quantise(yv_codes[n], yv_scales[n], yv_grouped[n], 0, CHANNELS)
 
         def flip_probabilities(n, t):
             if t == 0:
@@ -219,11 +220,11 @@ def tile_interral_pa_kernel(tc, xq, yk, y_feat, x_feat, W_v, b_v, out):
 
         def scale_columns(n, j):
             if j == 0:
-                attn_grouped[n] = grouped_pool.tile([P, ENTRIES, PACK], BF16, name="attn_grouped", align_bytes=64)
+                attn_grouped[n] = attn_pool.tile([P, ENTRIES, PACK], BF16, name="attn_grouped", align_bytes=64)
                 attn_codes[n] = mx_pool.tile([P, ENTRIES], U32, name="attn_codes", align_bytes=64)
                 attn_scales[n] = mx_pool.tile([P, ENTRIES], U8, name="attn_scales", align_bytes=64)
             queries = slice(j * P, (j + 1) * P)
-            nc.vector.tensor_tensor(
+            nc.gpsimd.tensor_tensor(
                 out=attn_grouped[n][:, queries, :],
                 in0=prob_t[n][:, :, queries].rearrange("p t b -> p b t"),
                 in1=col_inv[n][:].unsqueeze(1).to_broadcast([P, P, PACK]),
@@ -231,7 +232,8 @@ def tile_interral_pa_kernel(tc, xq, yk, y_feat, x_feat, W_v, b_v, out):
             )
 
         def quantise_attention(n, j):
-            quantise(attn_codes[n], attn_scales[n], attn_grouped[n], j * P, P)
+            if j == 0:
+                quantise(attn_codes[n], attn_scales[n], attn_grouped[n], 0, ENTRIES)
 
         def subtract_attended(n, j):
             queries = slice(j * P, (j + 1) * P)
@@ -262,13 +264,13 @@ def tile_interral_pa_kernel(tc, xq, yk, y_feat, x_feat, W_v, b_v, out):
                 run(scale_rows, tick - 1)
                 run(energy_softmax, tick)
                 run(invert_column_sums, tick - COLUMNS_DELAY)
+                run(quantise_weights, tick - 2, PACK)
+                run(quantise_features, tick - PACK)
+                run(quantise_values, tick - OUTPUT_DELAY)
+                run(quantise_attention, tick - OUTPUT_DELAY)
                 run(project_values, tick - VALUES_DELAY)
-                run(quantise_attention, tick - QUANTISE_DELAY)
                 run(subtract_attended, tick - OUTPUT_DELAY)
                 run(scale_columns, tick - COLUMNS_DELAY)
-                run(quantise_values, tick - VALUES_DELAY - 1)
-                run(quantise_features, tick - 1)
-                run(quantise_weights, tick - 1, PACK)
                 run(flip_probabilities, tick - FLIP_DELAY)
                 run(prepare_projections, tick + PROJECTIONS_LEAD)
                 run(prepare_features, tick)

@@ -101,7 +101,7 @@ def tile_interral_pa_kernel(tc, xq, yk, y_feat, x_feat, W_v, b_v, out):
                     nc.tensor.transpose(
                         flipped[:, g, u, :], words[:, 2 * pair + g, u * P : (u + 1) * P], ident_f32[:]
                     )
-            nc.scalar.copy(
+            nc.vector.tensor_copy(
                 out=grouped_words[:, 2 * pair : 2 * pair + 2],
                 in_=flipped[:].rearrange("q g u r -> q g r u"),
             )
@@ -110,7 +110,7 @@ def tile_interral_pa_kernel(tc, xq, yk, y_feat, x_feat, W_v, b_v, out):
             flipped = psum_flip.tile([P, PACK, P], BF16, tag="flip")
             for g in range(PACK):
                 nc.tensor.transpose(flipped[:, g, :], rows_sb[:, g, :], ident_bf16[:])
-            nc.scalar.copy(out=columns[:], in_=flipped[:].rearrange("d g r -> d (g r)"))
+            nc.vector.tensor_copy(out=columns[:], in_=flipped[:].rearrange("d g r -> d (g r)"))
 
         def prepare_projections(n, j):
             if j == 0:

@@ -101,7 +101,7 @@ def tile_interral_pa_kernel(tc, xq, yk, y_feat, x_feat, W_v, b_v, out):
                     nc.tensor.transpose(
                         flipped[:, g, u, :], words[:, 2 * pair + g, u * P : (u + 1) * P], ident_f32[:]
                     )
-            nc.vector.tensor_copy(
+            nc.scalar.copy(
                 out=grouped_words[:, 2 * pair : 2 * pair + 2],
                 in_=flipped[:].rearrange("q g u r -> q g r u"),
             )
@@ -110,7 +110,7 @@ def tile_interral_pa_kernel(tc, xq, yk, y_feat, x_feat, W_v, b_v, out):
             flipped = psum_flip.tile([P, PACK, P], BF16, tag="flip")
             for g in range(PACK):
                 nc.tensor.transpose(flipped[:, g, :], rows_sb[:, g, :], ident_bf16[:])
-            nc.vector.tensor_copy(out=columns[:], in_=flipped[:].rearrange("d g r -> d (g r)"))
+            nc.scalar.copy(out=columns[:], in_=flipped[:].rearrange("d g r -> d (g r)"))
 
         def prepare_projections(n, j):
             if j == 0:
@@ -224,7 +224,8 @@ def tile_interral_pa_kernel(tc, xq, yk, y_feat, x_feat, W_v, b_v, out):
                 attn_codes[n] = mx_pool.tile([P, ENTRIES], U32, name="attn_codes", align_bytes=64)
                 attn_scales[n] = mx_pool.tile([P, ENTRIES], U8, name="attn_scales", align_bytes=64)
             queries = slice(j * P, (j + 1) * P)
-            nc.gpsimd.tensor_tensor(
+            engine = nc.gpsimd if j % 2 == 0 else nc.vector
+            engine.tensor_tensor(
                 out=attn_grouped[n][:, queries, :],
                 in0=prob_t[n][:, :, queries].rearrange("p t b -> p b t"),
                 in1=col_inv[n][:].unsqueeze(1).to_broadcast([P, P, PACK]),

@@ -23,10 +23,13 @@ FLOPS = 2 * POINTS * ENTRIES * (CHANNELS * CHANNELS + ENTRIES * QK + ENTRIES * C
 
 
 PROJECTIONS_LEAD = 4
-VALUES_DELAY = 5
+FEATURES_QUANTISE_DELAY = 5
+VALUES_DELAY = 6
+VALUES_QUANTISE_DELAY = 10
 FLIP_DELAY = 4
 COLUMNS_DELAY = 8
-OUTPUT_DELAY = 12
+ATTENTION_QUANTISE_DELAY = 12
+OUTPUT_DELAY = 13
 QUARTERS = POINTS * PACK
 
 
@@ -224,8 +227,7 @@ def tile_interral_pa_kernel(tc, xq, yk, y_feat, x_feat, W_v, b_v, out):
                 attn_codes[n] = mx_pool.tile([P, ENTRIES], U32, name="attn_codes", align_bytes=64)
                 attn_scales[n] = mx_pool.tile([P, ENTRIES], U8, name="attn_scales", align_bytes=64)
             queries = slice(j * P, (j + 1) * P)
-            engine = nc.gpsimd if j % 2 == 0 else nc.vector
-            engine.tensor_tensor(
+            nc.gpsimd.tensor_tensor(
                 out=attn_grouped[n][:, queries, :],
                 in0=prob_t[n][:, :, queries].rearrange("p t b -> p b t"),
                 in1=col_inv[n][:].unsqueeze(1).to_broadcast([P, P, PACK]),
@@ -266,9 +268,9 @@ def tile_interral_pa_kernel(tc, xq, yk, y_feat, x_feat, W_v, b_v, out):
                 run(energy_softmax, tick)
                 run(invert_column_sums, tick - COLUMNS_DELAY)
                 run(quantise_weights, tick - 2, PACK)
-                run(quantise_features, tick - PACK)
-                run(quantise_values, tick - OUTPUT_DELAY)
-                run(quantise_attention, tick - OUTPUT_DELAY)
+                run(quantise_features, tick - FEATURES_QUANTISE_DELAY)
+                run(quantise_values, tick - VALUES_QUANTISE_DELAY)
+                run(quantise_attention, tick - ATTENTION_QUANTISE_DELAY)
                 run(project_values, tick - VALUES_DELAY)
                 run(subtract_attended, tick - OUTPUT_DELAY)
                 run(scale_columns, tick - COLUMNS_DELAY)

@@ -84,7 +84,7 @@ def tile_interral_pa_kernel(tc, xq, yk, y_feat, x_feat, W_v, b_v, out):
         xq_t, yk_t = {}, {}
         neg_max, row_sum, row_inv, prob = {}, {}, {}, {}
         yv_grouped, yv_codes, yv_scales = {}, {}, {}
-        col_sum, col_inv, prob_t = {}, {}, {}
+        col_sum, col_den, col_inv, prob_t = {}, {}, {}, {}
         attn_grouped, attn_codes, attn_scales = {}, {}, {}
 
         def quantise(codes, scales, grouped, first, count):
@@ -205,7 +205,6 @@ def tile_interral_pa_kernel(tc, xq, yk, y_feat, x_feat, W_v, b_v, out):
         def flip_probabilities(n, t):
             if t == 0:
                 col_sum[n] = stats.tile([P, PACK], F32, name="col_sum")
-                col_inv[n] = stats.tile([P, PACK], F32, name="col_inv")
                 prob_t[n] = soft.tile([P, PACK, ENTRIES], F32, name="prob_t")
             flipped_prob = psum_prob.tile([P, ENTRIES], F32)
             for j in range(PACK):
@@ -218,8 +217,10 @@ def tile_interral_pa_kernel(tc, xq, yk, y_feat, x_feat, W_v, b_v, out):
 
         def invert_column_sums(n, j):
             if j == 0:
-                nc.vector.tensor_scalar_add(out=col_inv[n][:], in0=col_sum[n][:], scalar1=EPS_L1)
-                nc.vector.reciprocal(out=col_inv[n][:], in_=col_inv[n][:])
+                col_den[n] = stats.tile([P, PACK], F32, name="col_den")
+                nc.vector.tensor_scalar_add(out=col_den[n][:], in0=col_sum[n][:], scalar1=EPS_L1)
+            col_inv[n, j] = stats.tile([P, PACK], F32, name="col_inv")
+            nc.vector.reciprocal(out=col_inv[n, j][:], in_=col_den[n][:])
 
         def scale_columns(n, j):
             if j == 0:
@@ -230,7 +231,7 @@ def tile_interral_pa_kernel(tc, xq, yk, y_feat, x_feat, W_v, b_v, out):
             nc.gpsimd.tensor_tensor(
                 out=attn_grouped[n][:, queries, :],
                 in0=prob_t[n][:, :, queries].rearrange("p t b -> p b t"),
-                in1=col_inv[n][:].unsqueeze(1).to_broadcast([P, P, PACK]),
+                in1=col_inv[n, j][:].unsqueeze(1).to_broadcast([P, P, PACK]),
                 op=ALU.mult,
             )
 
@@ -266,11 +267,11 @@ def tile_interral_pa_kernel(tc, xq, yk, y_feat, x_feat, W_v, b_v, out):
             for tick in range(-PROJECTIONS_LEAD, QUARTERS + OUTPUT_DELAY):
                 run(scale_rows, tick - 1)
                 run(energy_softmax, tick)
-                run(invert_column_sums, tick - COLUMNS_DELAY)
                 run(quantise_weights, tick - 2, PACK)
                 run(quantise_features, tick - FEATURES_QUANTISE_DELAY)
                 run(quantise_values, tick - VALUES_QUANTISE_DELAY)
                 run(quantise_attention, tick - ATTENTION_QUANTISE_DELAY)
+                run(invert_column_sums, tick - COLUMNS_DELAY)
                 run(project_values, tick - VALUES_DELAY)
                 run(subtract_attended, tick - OUTPUT_DELAY)
                 run(scale_columns, tick - COLUMNS_DELAY)

@@ -22,15 +22,18 @@ EPS_L1 = 1e-9
 FLOPS = 2 * POINTS * ENTRIES * (CHANNELS * CHANNELS + ENTRIES * QK + ENTRIES * CHANNELS)
 
 
-PROJECTIONS_LEAD = 4
-FEATURES_QUANTISE_DELAY = 5
-VALUES_DELAY = 6
-VALUES_QUANTISE_DELAY = 10
-FLIP_DELAY = 4
-COLUMNS_DELAY = 8
-ATTENTION_QUANTISE_DELAY = 12
-OUTPUT_DELAY = 13
 QUARTERS = POINTS * PACK
+WL = 1
+PROJ_LEAD = 4
+FEAT_LEAD = 0
+VALUES = 5
+VQ = 10
+FLIP = 6
+COL = 10
+AQ = 13
+OUT = 14
+EARLY_P = 2
+EARLY_F = 2
 
 
 def tile_interral_pa_kernel(tc, xq, yk, y_feat, x_feat, W_v, b_v, out):
@@ -39,11 +42,12 @@ def tile_interral_pa_kernel(tc, xq, yk, y_feat, x_feat, W_v, b_v, out):
         resident = ctx.enter_context(tc.tile_pool(name="resident", bufs=1))
         proj = ctx.enter_context(tc.tile_pool(name="proj", bufs=3))
         grouped_pool = ctx.enter_context(tc.tile_pool(name="grouped", bufs=2))
-        attn_pool = ctx.enter_context(tc.tile_pool(name="attn", bufs=1))
-        mx_pool = ctx.enter_context(tc.tile_pool(name="mx", bufs=3))
-        values_pool = ctx.enter_context(tc.tile_pool(name="values", bufs=4))
+        attn_pool = ctx.enter_context(tc.tile_pool(name="attn", bufs=2))
+        mx_pool = ctx.enter_context(tc.tile_pool(name="mx", bufs=2))
+        values_pool = ctx.enter_context(tc.tile_pool(name="values", bufs=5))
         soft = ctx.enter_context(tc.tile_pool(name="soft", bufs=3))
         stats = ctx.enter_context(tc.tile_pool(name="stats", bufs=4))
+        inv_pool = ctx.enter_context(tc.tile_pool(name="inv", bufs=8))
         result_pool = ctx.enter_context(tc.tile_pool(name="result", bufs=4))
         psum_flip = ctx.enter_context(tc.psum_pool(name="psum_flip", bufs=2))
         psum_energy = ctx.enter_context(tc.psum_pool(name="psum_energy", bufs=2))
@@ -71,9 +75,10 @@ def tile_interral_pa_kernel(tc, xq, yk, y_feat, x_feat, W_v, b_v, out):
             nc.sync.dma_start(out=y_sb[n][:], in_=y_rows[n])
             if n == 0:
                 nc.sync.dma_start(out=bias_sb[:], in_=b_v.partition_broadcast(P))
-            else:
-                nc.sync.dma_start(out=x_sb[n - 1][:], in_=x_rows[n - 1])
-        nc.sync.dma_start(out=x_sb[POINTS - 1][:], in_=x_rows[POINTS - 1])
+            elif n > 1:
+                nc.sync.dma_start(out=x_sb[n - 2][:], in_=x_rows[n - 2])
+        for n in (POINTS - 2, POINTS - 1):
+            nc.sync.dma_start(out=x_sb[n][:], in_=x_rows[n])
 
         ident_f32 = resident.tile([P, P], F32)
         make_identity(nc, ident_f32[:])
@@ -82,9 +87,11 @@ def tile_interral_pa_kernel(tc, xq, yk, y_feat, x_feat, W_v, b_v, out):
 
         y_grouped, y_codes, y_scales = {}, {}, {}
         xq_t, yk_t = {}, {}
-        neg_max, row_sum, row_inv, prob = {}, {}, {}, {}
+        energy = {}
+        neg_max, stat, inv, prob = {}, {}, {}, {}
         yv_grouped, yv_codes, yv_scales = {}, {}, {}
-        col_sum, col_den, col_inv, prob_t = {}, {}, {}, {}
+        yv_acc, yr_acc = {}, {}
+        col_sum, prob_t = {}, {}
         attn_grouped, attn_codes, attn_scales = {}, {}, {}
 
         def quantise(codes, scales, grouped, first, count):
@@ -95,41 +102,50 @@ def tile_interral_pa_kernel(tc, xq, yk, y_feat, x_feat, W_v, b_v, out):
                 in_=grouped[:, cols, :].rearrange("q r t -> q (r t)"),
             )
 
-        def channels_to_partitions(rows_sb, grouped, pair):
+        flipped = {}
+
+        def channels_to_partitions(rows_sb, key, pair):
             words = rows_sb[:].bitcast(F32)
-            grouped_words = grouped[:].bitcast(F32).rearrange("q (g r) u -> q g r u", g=PACK)
-            flipped = psum_flip.tile([P, 2, 2, P], F32, tag="flip")
+            flipped[key] = psum_flip.tile([P, 2, 2, P], F32, name="flipped", tag="flip")
             for g in range(2):
                 for u in range(2):
                     nc.tensor.transpose(
-                        flipped[:, g, u, :], words[:, 2 * pair + g, u * P : (u + 1) * P], ident_f32[:]
+                        flipped[key][:, g, u, :], words[:, 2 * pair + g, u * P : (u + 1) * P], ident_f32[:]
                     )
-            nc.scalar.copy(
+
+        def evacuate_channels(key, grouped, pair, copy):
+            grouped_words = grouped[:].bitcast(F32).rearrange("q (g r) u -> q g r u", g=PACK)
+            copy(
                 out=grouped_words[:, 2 * pair : 2 * pair + 2],
-                in_=flipped[:].rearrange("q g u r -> q g r u"),
+                in_=flipped[key][:].rearrange("q g u r -> q g r u"),
             )
 
-        def projection_to_partitions(rows_sb, columns):
-            flipped = psum_flip.tile([P, PACK, P], BF16, tag="flip")
-            for g in range(PACK):
-                nc.tensor.transpose(flipped[:, g, :], rows_sb[:, g, :], ident_bf16[:])
-            nc.scalar.copy(out=columns[:], in_=flipped[:].rearrange("d g r -> d (g r)"))
-
         def prepare_projections(n, j):
-            if j == 0:
-                xq_t[n] = proj.tile([P, ENTRIES], BF16, name="xq_t")
-                projection_to_partitions(xq_sb[n], xq_t[n])
-            elif j == 1:
-                yk_t[n] = proj.tile([P, ENTRIES], BF16, name="yk_t")
-                projection_to_partitions(yk_sb[n], yk_t[n])
+            if j < 2:
+                rows_sb = (xq_sb, yk_sb)[j][n]
+                flipped["p", n, j] = psum_flip.tile([P, PACK, P], BF16, name="flipped_p", tag="flip")
+                for g in range(PACK):
+                    nc.tensor.transpose(flipped["p", n, j][:, g, :], rows_sb[:, g, :], ident_bf16[:])
+
+        def evacuate_projections(n, j):
+            if j < 2:
+                copy = nc.vector.tensor_copy if (n, j) in ((0, 1), (1, 0), (1, 1)) else nc.scalar.copy
+                t = proj.tile([P, ENTRIES], BF16, name="proj%d" % j)
+                (xq_t, yk_t)[j][n] = t
+                copy(out=t[:], in_=flipped["p", n, j][:].rearrange("d g r -> d (g r)"))
 
         def prepare_features(n, j):
+            if j >= 2:
+                channels_to_partitions(y_sb[n], ("y", n, j), j - 2)
+
+        def evacuate_features(n, j):
             if j == 2:
                 y_grouped[n] = grouped_pool.tile([P, ENTRIES, PACK], BF16, name="y_grouped", align_bytes=64)
                 y_codes[n] = mx_pool.tile([P, ENTRIES], U32, name="y_codes", align_bytes=64)
                 y_scales[n] = mx_pool.tile([P, ENTRIES], U8, name="y_scales", align_bytes=64)
             if j >= 2:
-                channels_to_partitions(y_sb[n], y_grouped[n], j - 2)
+                copy = nc.vector.tensor_copy if (n, j) in ((0, 2), (0, 3), (1, 2), (1, 3)) else nc.scalar.copy
+                evacuate_channels(("y", n, j), y_grouped[n], j - 2, copy)
 
         def quantise_features(n, j):
             if j == 0:
@@ -137,53 +153,93 @@ def tile_interral_pa_kernel(tc, xq, yk, y_feat, x_feat, W_v, b_v, out):
 
         def prepare_weights(n, j):
             if j < 2:
-                channels_to_partitions(w_sb, w_grouped, j)
+                channels_to_partitions(w_sb, ("w", j), j)
+
+        def evacuate_weights(n, j):
+            if j < 2:
+                evacuate_channels(("w", j), w_grouped, j, nc.vector.tensor_copy if True else nc.scalar.copy)
 
         def quantise_weights(n, j):
             if j == 0:
                 quantise(w_codes, w_scales, w_grouped, 0, CHANNELS)
 
-        def energy_softmax(n, j):
+        def energies(n, j):
+            energy[n, j] = psum_energy.tile([P, ENTRIES], F32, name="energy")
+            nc.tensor.matmul(
+                out=energy[n, j][:], lhsT=xq_t[n][:, j * P : (j + 1) * P], rhs=yk_t[n][:], start=True, stop=True
+            )
+
+        def row_max(n, j):
             if j == 0:
                 neg_max[n] = stats.tile([P, PACK], F32, name="neg_max")
-                row_sum[n] = stats.tile([P, PACK], F32, name="row_sum")
-                row_inv[n] = stats.tile([P, PACK], F32, name="row_inv")
                 prob[n] = soft.tile([P, PACK, ENTRIES], F32, name="prob")
-            energy = psum_energy.tile([P, ENTRIES], F32)
-            nc.tensor.matmul(
-                out=energy[:], lhsT=xq_t[n][:, j * P : (j + 1) * P], rhs=yk_t[n][:], start=True, stop=True
-            )
             nc.vector.tensor_reduce(
-                out=neg_max[n][:, j : j + 1], in_=energy[:], axis=mybir.AxisListType.X, op=ALU.max, negate=True
+                out=neg_max[n][:, j : j + 1], in_=energy[n, j][:], axis=mybir.AxisListType.X, op=ALU.max, negate=True
             )
+
+        def stat_of(i):
+            q = (i + 3) // PACK
+            if q not in stat:
+                stat[q] = stats.tile([P, 2 * PACK], F32, name="stat")
+            return q, PACK + (i + 3) % PACK
+
+        def exponentials(n, j):
+            q, c = stat_of(PACK * n + j)
             nc.scalar.activation(
                 out=prob[n][:, j, :],
-                in_=energy[:],
+                in_=energy[n, j][:],
                 func=ACT.Exp,
                 bias=neg_max[n][:, j : j + 1],
                 scale=1.0,
-                accum_out=row_sum[n][:, j : j + 1],
+                accum_out=stat[q][:, c : c + 1],
             )
 
-        def invert_row_sums(n, j):
-            nc.vector.reciprocal(out=row_inv[n][:, j : j + 1], in_=row_sum[n][:, j : j + 1])
+        def invert(m, j):
+            i = PACK * m + j
+            q, c = stat_of(i)
+            first, last = (PACK if i > 0 else 2 * PACK - 1), PACK
+            n = (i + 1 - COL) // PACK
+            if 0 <= n < POINTS:
+                first = 0
+                if (i + 1 - COL) % PACK == 0:
+                    nc.vector.tensor_scalar_add(out=stat[q][:, 0:PACK], in0=col_sum[n][:], scalar1=EPS_L1)
+            if i < QUARTERS:
+                last = c + 1
+            if last > first:
+                inv[i] = inv_pool.tile([P, 2 * PACK], F32, name="inv")
+                nc.vector.reciprocal(out=inv[i][:, first:last], in_=stat[q][:, first:last])
+
+        diagonal = {}
+
+        def build_diagonal(n, j):
+            how = ROW[(n, j)] if (n, j) in ROW else ROW[j]
+            if how == "D":
+                q, c = stat_of(PACK * n + j)
+                diagonal[n, j] = stats.tile([P, P], F32, name="diagonal", bufs=6)
+                nc.gpsimd.tensor_scalar(out=diagonal[n, j][:], in0=ident_f32[:], scalar1=inv[PACK * n + j][:, c : c + 1], scalar2=0.0, op0=ALU.mult, op1=ALU.add)
 
         def scale_rows(n, j):
-            nc.scalar.activation(
-                out=prob[n][:, j, :], in_=prob[n][:, j, :], func=ACT.Copy, scale=row_inv[n][:, j : j + 1]
-            )
+            q, c = stat_of(PACK * n + j)
+            scale = inv[PACK * n + j][:, c : c + 1]
+            how = ROW[(n, j)] if (n, j) in ROW else ROW[j]
+            if how == "S":
+                nc.scalar.activation(out=prob[n][:, j, :], in_=prob[n][:, j, :], func=ACT.Copy, scale=scale)
+            elif how == "V":
+                nc.vector.tensor_scalar_mul(out=prob[n][:, j, :], in0=prob[n][:, j, :], scalar1=scale)
+            elif how == "G":
+                nc.gpsimd.tensor_scalar(out=prob[n][:, j, :], in0=prob[n][:, j, :], scalar1=scale, scalar2=0.0, op0=ALU.mult, op1=ALU.add)
 
-        def project_values(n, c):
+        def values_mx(n, c):
             if c == 0:
                 yv_grouped[n] = grouped_pool.tile([P, CHANNELS, PACK], BF16, name="yv_grouped", align_bytes=64)
                 yv_codes[n] = values_pool.tile([P, CHANNELS], U32, name="yv_codes", align_bytes=64)
                 yv_scales[n] = values_pool.tile([P, CHANNELS], U8, name="yv_scales", align_bytes=64)
             cols = slice(c * P, (c + 1) * P)
-            yv_acc = psum_mx.tile([P, PACK, P], F32, tag="acc")
+            yv_acc[n, c] = psum_mx.tile([P, PACK, P], F32, name="yv_acc", tag="acc")
             for t in range(PACK):
                 keys = slice(t * P, (t + 1) * P)
                 nc.tensor.matmul_mx(
-                    out=yv_acc[:, t, :],
+                    out=yv_acc[n, c][:, t, :],
                     lhsT=y_codes[n][:, keys].bitcast(FP8X4),
                     lhsT_scale=y_scales[n][:, keys],
                     rhs=w_codes[:, cols].bitcast(FP8X4),
@@ -191,9 +247,12 @@ def tile_interral_pa_kernel(tc, xq, yk, y_feat, x_feat, W_v, b_v, out):
                     start=True,
                     stop=True,
                 )
+
+        def add_bias(n, c):
+            cols = slice(c * P, (c + 1) * P)
             nc.vector.tensor_tensor(
                 out=yv_grouped[n][:, cols, :],
-                in0=yv_acc[:].rearrange("p t c -> p c t"),
+                in0=yv_acc[n, c][:].rearrange("p t c -> p c t"),
                 in1=bias_sb[:, cols].unsqueeze(2).to_broadcast([P, P, PACK]),
                 op=ALU.add,
             )
@@ -202,25 +261,28 @@ def tile_interral_pa_kernel(tc, xq, yk, y_feat, x_feat, W_v, b_v, out):
             if j == 0:
                 quantise(yv_codes[n], yv_scales[n], yv_grouped[n], 0, CHANNELS)
 
+        flipped_prob = {}
+
         def flip_probabilities(n, t):
             if t == 0:
                 col_sum[n] = stats.tile([P, PACK], F32, name="col_sum")
-                prob_t[n] = soft.tile([P, PACK, ENTRIES], F32, name="prob_t")
-            flipped_prob = psum_prob.tile([P, ENTRIES], F32)
+                prob_t[n] = soft.tile([P, PACK, ENTRIES], F32, name="prob_t", bufs=2)
+            flipped_prob[n, t] = psum_prob.tile([P, ENTRIES], F32, name="flipped_prob")
             for j in range(PACK):
-                nc.tensor.transpose(
-                    flipped_prob[:, j * P : (j + 1) * P], prob[n][:, j, t * P : (t + 1) * P], ident_f32[:]
-                )
-            nc.scalar.activation(
-                out=prob_t[n][:, t, :], in_=flipped_prob[:], func=ACT.Copy, accum_out=col_sum[n][:, t : t + 1]
-            )
+                target = flipped_prob[n, t][:, j * P : (j + 1) * P]
+                source = prob[n][:, j, t * P : (t + 1) * P]
+                if (n, j) in diagonal:
+                    nc.tensor.matmul(out=target, lhsT=source, rhs=diagonal[n, j][:], start=True, stop=True)
+                else:
+                    nc.tensor.transpose(target, source, ident_f32[:])
 
-        def invert_column_sums(n, j):
-            if j == 0:
-                col_den[n] = stats.tile([P, PACK], F32, name="col_den")
-                nc.vector.tensor_scalar_add(out=col_den[n][:], in0=col_sum[n][:], scalar1=EPS_L1)
-            col_inv[n, j] = stats.tile([P, PACK], F32, name="col_inv")
-            nc.vector.reciprocal(out=col_inv[n, j][:], in_=col_den[n][:])
+        def sum_columns(n, t):
+            if n == POINTS - 1 and t % 2 == 1 and 0:
+                nc.vector.tensor_scalar(out=prob_t[n][:, t, :], in0=flipped_prob[n, t][:], scalar1=1.0, scalar2=None, op0=ALU.mult, op1=ALU.add, accum_out=col_sum[n][:, t : t + 1])
+            else:
+                nc.scalar.activation(
+                    out=prob_t[n][:, t, :], in_=flipped_prob[n, t][:], func=ACT.Copy, accum_out=col_sum[n][:, t : t + 1]
+                )
 
         def scale_columns(n, j):
             if j == 0:
@@ -228,10 +290,11 @@ def tile_interral_pa_kernel(tc, xq, yk, y_feat, x_feat, W_v, b_v, out):
                 attn_codes[n] = mx_pool.tile([P, ENTRIES], U32, name="attn_codes", align_bytes=64)
                 attn_scales[n] = mx_pool.tile([P, ENTRIES], U8, name="attn_scales", align_bytes=64)
             queries = slice(j * P, (j + 1) * P)
-            nc.gpsimd.tensor_tensor(
+            engine = nc.vector if n == POINTS - 1 and j in (0,1,2,3) else nc.gpsimd
+            engine.tensor_tensor(
                 out=attn_grouped[n][:, queries, :],
                 in0=prob_t[n][:, :, queries].rearrange("p t b -> p b t"),
-                in1=col_inv[n, j][:].unsqueeze(1).to_broadcast([P, P, PACK]),
+                in1=inv[PACK * n + j + COL - 1][:, 0:PACK].unsqueeze(1).to_broadcast([P, P, PACK]),
                 op=ALU.mult,
             )
 
@@ -239,11 +302,11 @@ def tile_interral_pa_kernel(tc, xq, yk, y_feat, x_feat, W_v, b_v, out):
             if j == 0:
                 quantise(attn_codes[n], attn_scales[n], attn_grouped[n], 0, ENTRIES)
 
-        def subtract_attended(n, j):
+        def output_mx(n, j):
             queries = slice(j * P, (j + 1) * P)
-            yr_acc = psum_mx.tile([P, CHANNELS], F32, tag="acc")
+            yr_acc[n, j] = psum_mx.tile([P, CHANNELS], F32, name="yr_acc", tag="acc")
             nc.tensor.matmul_mx(
-                out=yr_acc[:],
+                out=yr_acc[n, j][:],
                 lhsT=attn_codes[n][:, queries].bitcast(FP8X4),
                 lhsT_scale=attn_scales[n][:, queries],
                 rhs=yv_codes[n][:].bitcast(FP8X4),
@@ -251,9 +314,19 @@ def tile_interral_pa_kernel(tc, xq, yk, y_feat, x_feat, W_v, b_v, out):
                 start=True,
                 stop=True,
             )
+
+        def subtract_attended(n, j):
             result = result_pool.tile([P, CHANNELS], F32)
-            nc.vector.tensor_tensor(out=result[:], in0=x_sb[n][:, j, :], in1=yr_acc[:], op=ALU.subtract)
+            if (n, j) in SUBG or j in SUBG:
+                staged = result_pool.tile([P, CHANNELS], F32, name="staged", bufs=2)
+                nc.scalar.copy(out=staged[:], in_=yr_acc[n, j][:])
+                nc.gpsimd.tensor_tensor(out=result[:], in0=x_sb[n][:, j, :], in1=staged[:], op=ALU.subtract)
+            else:
+                nc.vector.tensor_tensor(out=result[:], in0=x_sb[n][:, j, :], in1=yr_acc[n, j][:], op=ALU.subtract)
             nc.sync.dma_start(out=out_rows[n, j], in_=result[:])
+
+        ROW = {0: "D", 1: "S", 2: "D", 3: "S"}
+        SUBG = ()
 
         def run(stage, index, count=QUARTERS):
             if 0 <= index < count:
@@ -264,19 +337,27 @@ def tile_interral_pa_kernel(tc, xq, yk, y_feat, x_feat, W_v, b_v, out):
         w_scales = resident.tile([P, CHANNELS], U8, align_bytes=64)
 
         with tc.manual_schedule():
-            for tick in range(-PROJECTIONS_LEAD, QUARTERS + OUTPUT_DELAY):
+            for tick in range(-PROJ_LEAD - 1, QUARTERS + OUT):
+                run(invert, tick - 1, QUARTERS + 4 * PACK)
+                run(row_max, tick)
+                run(build_diagonal, tick - 1)
+                run(sum_columns, tick - FLIP)
+                run(exponentials, tick)
                 run(scale_rows, tick - 1)
-                run(energy_softmax, tick)
-                run(quantise_weights, tick - 2, PACK)
-                run(quantise_features, tick - FEATURES_QUANTISE_DELAY)
-                run(quantise_values, tick - VALUES_QUANTISE_DELAY)
-                run(quantise_attention, tick - ATTENTION_QUANTISE_DELAY)
-                run(invert_column_sums, tick - COLUMNS_DELAY)
-                run(project_values, tick - VALUES_DELAY)
-                run(subtract_attended, tick - OUTPUT_DELAY)
-                run(scale_columns, tick - COLUMNS_DELAY)
-                run(flip_probabilities, tick - FLIP_DELAY)
-                run(prepare_projections, tick + PROJECTIONS_LEAD)
-                run(prepare_features, tick)
-                run(prepare_weights, tick, PACK)
-                run(invert_row_sums, tick)
+                run(scale_columns, tick - COL)
+                run(subtract_attended, tick - OUT)
+                run(add_bias, tick - VALUES)
+                run(evacuate_projections, tick + PROJ_LEAD)
+                run(evacuate_weights, tick + WL, PACK)
+                run(evacuate_features, tick + FEAT_LEAD)
+                run(quantise_weights, tick + WL - 2, PACK)
+                run(quantise_features, tick + FEAT_LEAD - 4)
+                run(quantise_values, tick - VQ)
+                run(quantise_attention, tick - AQ)
+                run(energies, tick + 1)
+                run(flip_probabilities, tick + 1 - FLIP)
+                run(prepare_projections, tick + PROJ_LEAD + 1)
+                run(prepare_weights, tick + WL + 1, PACK)
+                run(prepare_features, tick + FEAT_LEAD + 1)
+                run(output_mx, tick + 1 - OUT)
+                run(values_mx, tick + 1 - VALUES)

@@ -27,10 +27,10 @@ WL = 1
 PROJ_LEAD = 4
 FEAT_LEAD = 0
 VALUES = 5
-VQ = 10
+VQ = 11
 FLIP = 6
 COL = 10
-AQ = 13
+AQ = 14
 OUT = 14
 EARLY_P = 2
 EARLY_F = 2
@@ -49,9 +49,8 @@ def tile_interral_pa_kernel(tc, xq, yk, y_feat, x_feat, W_v, b_v, out):
         stats = ctx.enter_context(tc.tile_pool(name="stats", bufs=4))
         inv_pool = ctx.enter_context(tc.tile_pool(name="inv", bufs=8))
         result_pool = ctx.enter_context(tc.tile_pool(name="result", bufs=4))
-        psum_flip = ctx.enter_context(tc.psum_pool(name="psum_flip", bufs=2))
+        psum_flip = ctx.enter_context(tc.psum_pool(name="psum_flip", bufs=4))
         psum_energy = ctx.enter_context(tc.psum_pool(name="psum_energy", bufs=2))
-        psum_prob = ctx.enter_context(tc.psum_pool(name="psum_prob", bufs=2))
         psum_mx = ctx.enter_context(tc.psum_pool(name="psum_mx", bufs=2))
 
         xq_rows = xq.rearrange("n (p g) d -> n p g d", g=PACK)
@@ -94,6 +93,14 @@ def tile_interral_pa_kernel(tc, xq, yk, y_feat, x_feat, W_v, b_v, out):
         col_sum, prob_t = {}, {}
         attn_grouped, attn_codes, attn_scales = {}, {}, {}
 
+        bias_column = resident.tile([P, PACK], F32)
+
+        def prepare_bias():
+            turned = psum_flip.tile([P, PACK, P], BF16, name="flipped_p", tag="flip")
+            for c in range(PACK):
+                nc.tensor.transpose(turned[:, c, :], bias_sb[:, c * P : (c + 1) * P], ident_bf16[:])
+            nc.vector.tensor_copy(out=bias_column[:], in_=turned[:, :, 0])
+
         def quantise(codes, scales, grouped, first, count):
             cols = slice(first, first + count)
             nc.vector.quantize_mx(
@@ -129,7 +136,7 @@ def tile_interral_pa_kernel(tc, xq, yk, y_feat, x_feat, W_v, b_v, out):
 
         def evacuate_projections(n, j):
             if j < 2:
-                copy = nc.vector.tensor_copy if (n, j) in ((0, 1), (1, 0), (1, 1)) else nc.scalar.copy
+                copy = nc.vector.tensor_copy if n < 2 and (n, j) != (0, 0) else nc.scalar.copy
                 t = proj.tile([P, ENTRIES], BF16, name="proj%d" % j)
                 (xq_t, yk_t)[j][n] = t
                 copy(out=t[:], in_=flipped["p", n, j][:].rearrange("d g r -> d (g r)"))
@@ -144,7 +151,7 @@ def tile_interral_pa_kernel(tc, xq, yk, y_feat, x_feat, W_v, b_v, out):
                 y_codes[n] = mx_pool.tile([P, ENTRIES], U32, name="y_codes", align_bytes=64)
                 y_scales[n] = mx_pool.tile([P, ENTRIES], U8, name="y_scales", align_bytes=64)
             if j >= 2:
-                copy = nc.vector.tensor_copy if (n, j) in ((0, 2), (0, 3), (1, 2), (1, 3)) else nc.scalar.copy
+                copy = nc.vector.tensor_copy if n < 2 else nc.scalar.copy
                 evacuate_channels(("y", n, j), y_grouped[n], j - 2, copy)
 
         def quantise_features(n, j):
@@ -236,6 +243,17 @@ def tile_interral_pa_kernel(tc, xq, yk, y_feat, x_feat, W_v, b_v, out):
                 yv_scales[n] = values_pool.tile([P, CHANNELS], U8, name="yv_scales", align_bytes=64)
             cols = slice(c * P, (c + 1) * P)
             yv_acc[n, c] = psum_mx.tile([P, PACK, P], F32, name="yv_acc", tag="acc")
+            if False:
+                nc.tensor.matmul_mx(
+                    out=yv_acc[n, c][:].rearrange("p t c -> p (t c)"),
+                    lhsT=w_codes[:, cols].bitcast(FP8X4),
+                    lhsT_scale=w_scales[:, cols],
+                    rhs=y_codes[n][:].bitcast(FP8X4),
+                    rhs_scale=y_scales[n][:],
+                    start=True,
+                    stop=True,
+                )
+                return
             for t in range(PACK):
                 keys = slice(t * P, (t + 1) * P)
                 nc.tensor.matmul_mx(
@@ -248,7 +266,36 @@ def tile_interral_pa_kernel(tc, xq, yk, y_feat, x_feat, W_v, b_v, out):
                     stop=True,
                 )
 
+        yv_turned, yv_words = {}, {}
+
+        def add_bias_turned(n, c):
+            if False:
+                yv_turned[n, c] = soft.tile([P, 2, P, 2], BF16, name="yv_turned", bufs=2)
+                nc.scalar.activation(
+                    out=yv_turned[n, c][:],
+                    in_=yv_acc[n, c][:].rearrange("c (u e) p -> c u p e", u=2),
+                    func=ACT.Identity,
+                    bias=bias_column[:, c : c + 1],
+                    scale=1.0,
+                )
+
+        def flip_values(n, c):
+            if False:
+                words = yv_turned[n, c][:].rearrange("c u p e -> c (u p e)").bitcast(F32)
+                yv_words[n, c] = psum_flip.tile([P, 2, P], F32, name="yv_words", tag="flip")
+                for u in range(2):
+                    nc.tensor.transpose(yv_words[n, c][:, u, :], words[:, u * P : (u + 1) * P], ident_f32[:])
+
+        def evacuate_values(n, c):
+            if False:
+                grouped_words = yv_grouped[n][:].bitcast(F32)
+                nc.scalar.copy(
+                    out=grouped_words[:, c * P : (c + 1) * P, :], in_=yv_words[n, c][:].rearrange("p u c -> p c u")
+                )
+
         def add_bias(n, c):
+            if False:
+                return
             cols = slice(c * P, (c + 1) * P)
             nc.vector.tensor_tensor(
                 out=yv_grouped[n][:, cols, :],
@@ -267,7 +314,7 @@ def tile_interral_pa_kernel(tc, xq, yk, y_feat, x_feat, W_v, b_v, out):
             if t == 0:
                 col_sum[n] = stats.tile([P, PACK], F32, name="col_sum")
                 prob_t[n] = soft.tile([P, PACK, ENTRIES], F32, name="prob_t", bufs=2)
-            flipped_prob[n, t] = psum_prob.tile([P, ENTRIES], F32, name="flipped_prob")
+            flipped_prob[n, t] = psum_flip.tile([P, ENTRIES], F32, name="flipped_prob", tag="flip")
             for j in range(PACK):
                 target = flipped_prob[n, t][:, j * P : (j + 1) * P]
                 source = prob[n][:, j, t * P : (t + 1) * P]
@@ -290,7 +337,7 @@ def tile_interral_pa_kernel(tc, xq, yk, y_feat, x_feat, W_v, b_v, out):
                 attn_codes[n] = mx_pool.tile([P, ENTRIES], U32, name="attn_codes", align_bytes=64)
                 attn_scales[n] = mx_pool.tile([P, ENTRIES], U8, name="attn_scales", align_bytes=64)
             queries = slice(j * P, (j + 1) * P)
-            engine = nc.vector if n == POINTS - 1 and j in (0,1,2,3) else nc.gpsimd
+            engine = nc.vector if n == POINTS - 1 and j in () else nc.gpsimd
             engine.tensor_tensor(
                 out=attn_grouped[n][:, queries, :],
                 in0=prob_t[n][:, :, queries].rearrange("p t b -> p b t"),
@@ -325,7 +372,7 @@ def tile_interral_pa_kernel(tc, xq, yk, y_feat, x_feat, W_v, b_v, out):
                 nc.vector.tensor_tensor(out=result[:], in0=x_sb[n][:, j, :], in1=yr_acc[n, j][:], op=ALU.subtract)
             nc.sync.dma_start(out=out_rows[n, j], in_=result[:])
 
-        ROW = {0: "D", 1: "S", 2: "D", 3: "S"}
+        ROW = {0: "S", 1: "S", 2: "S", 3: "S"}
         SUBG = ()
 
         def run(stage, index, count=QUARTERS):
@@ -338,26 +385,31 @@ def tile_interral_pa_kernel(tc, xq, yk, y_feat, x_feat, W_v, b_v, out):
 
         with tc.manual_schedule():
             for tick in range(-PROJ_LEAD - 1, QUARTERS + OUT):
-                run(invert, tick - 1, QUARTERS + 4 * PACK)
                 run(row_max, tick)
+                run(quantise_weights, tick + WL - 2, PACK)
+                run(quantise_features, tick + FEAT_LEAD - 4)
+                run(quantise_values, tick - VQ)
+                run(quantise_attention, tick - AQ)
+                run(invert, tick - 1, QUARTERS + 4 * PACK)
                 run(build_diagonal, tick - 1)
                 run(sum_columns, tick - FLIP)
                 run(exponentials, tick)
                 run(scale_rows, tick - 1)
                 run(scale_columns, tick - COL)
-                run(subtract_attended, tick - OUT)
-                run(add_bias, tick - VALUES)
                 run(evacuate_projections, tick + PROJ_LEAD)
                 run(evacuate_weights, tick + WL, PACK)
                 run(evacuate_features, tick + FEAT_LEAD)
-                run(quantise_weights, tick + WL - 2, PACK)
-                run(quantise_features, tick + FEAT_LEAD - 4)
-                run(quantise_values, tick - VQ)
-                run(quantise_attention, tick - AQ)
+                run(add_bias, tick - VALUES)
+                run(add_bias_turned, tick - VALUES)
+                run(evacuate_values, tick - VALUES - 2)
+                run(output_mx, tick - OUT)
+                run(subtract_attended, tick - OUT)
                 run(energies, tick + 1)
                 run(flip_probabilities, tick + 1 - FLIP)
+                run(flip_values, tick - VALUES - 1)
                 run(prepare_projections, tick + PROJ_LEAD + 1)
                 run(prepare_weights, tick + WL + 1, PACK)
                 run(prepare_features, tick + FEAT_LEAD + 1)
-                run(output_mx, tick + 1 - OUT)
+                if tick == -1:
+                    prepare_bias()
                 run(values_mx, tick + 1 - VALUES)

@@ -339,9 +339,9 @@ def tile_interral_pa_kernel(tc, xq, yk, y_feat, x_feat, W_v, b_v, out):
             queries = slice(j * P, (j + 1) * P)
             engine = nc.vector if n == POINTS - 1 and j in () else nc.gpsimd
             engine.tensor_tensor(
-                out=attn_grouped[n][:, queries, :],
-                in0=prob_t[n][:, :, queries].rearrange("p t b -> p b t"),
-                in1=inv[PACK * n + j + COL - 1][:, 0:PACK].unsqueeze(1).to_broadcast([P, P, PACK]),
+                out=attn_grouped[n][:, queries, :].rearrange("p (b i) t -> p b t i", i=4),
+                in0=prob_t[n][:, :, queries].rearrange("p t (b i) -> p b t i", i=4),
+                in1=inv[PACK * n + j + COL - 1][:, 0:PACK].unsqueeze(1).unsqueeze(3).to_broadcast([P, P // 4, PACK, 4]),
                 op=ALU.mult,
             )
 

@@ -23,7 +23,7 @@ FLOPS = 2 * POINTS * ENTRIES * (CHANNELS * CHANNELS + ENTRIES * QK + ENTRIES * C
 
 
 QUARTERS = POINTS * PACK
-WL = 1
+WL = -1
 PROJ_LEAD = 4
 FEAT_LEAD = 0
 VALUES = 5
@@ -136,7 +136,7 @@ def tile_interral_pa_kernel(tc, xq, yk, y_feat, x_feat, W_v, b_v, out):
 
         def evacuate_projections(n, j):
             if j < 2:
-                copy = nc.vector.tensor_copy if n < 2 and (n, j) != (0, 0) else nc.scalar.copy
+                copy = nc.vector.tensor_copy if n < 3 and (n, j) != (0, 0) else nc.scalar.copy
                 t = proj.tile([P, ENTRIES], BF16, name="proj%d" % j)
                 (xq_t, yk_t)[j][n] = t
                 copy(out=t[:], in_=flipped["p", n, j][:].rearrange("d g r -> d (g r)"))
@@ -151,7 +151,7 @@ def tile_interral_pa_kernel(tc, xq, yk, y_feat, x_feat, W_v, b_v, out):
                 y_codes[n] = mx_pool.tile([P, ENTRIES], U32, name="y_codes", align_bytes=64)
                 y_scales[n] = mx_pool.tile([P, ENTRIES], U8, name="y_scales", align_bytes=64)
             if j >= 2:
-                copy = nc.vector.tensor_copy if n < 2 else nc.scalar.copy
+                copy = nc.vector.tensor_copy if n < 3 else nc.scalar.copy
                 evacuate_channels(("y", n, j), y_grouped[n], j - 2, copy)
 
         def quantise_features(n, j):
@@ -313,7 +313,7 @@ def tile_interral_pa_kernel(tc, xq, yk, y_feat, x_feat, W_v, b_v, out):
         def flip_probabilities(n, t):
             if t == 0:
                 col_sum[n] = stats.tile([P, PACK], F32, name="col_sum")
-                prob_t[n] = soft.tile([P, PACK, ENTRIES], F32, name="prob_t", bufs=2)
+                prob_t[n] = soft.tile([P, PACK, ENTRIES], F32, name="prob_t", bufs=3)
             flipped_prob[n, t] = psum_flip.tile([P, ENTRIES], F32, name="flipped_prob", tag="flip")
             for j in range(PACK):
                 target = flipped_prob[n, t][:, j * P : (j + 1) * P]
@@ -331,17 +331,27 @@ def tile_interral_pa_kernel(tc, xq, yk, y_feat, x_feat, W_v, b_v, out):
                     out=prob_t[n][:, t, :], in_=flipped_prob[n, t][:], func=ACT.Copy, accum_out=col_sum[n][:, t : t + 1]
                 )
 
+        def on_vector(n, j):
+            return j == 3
+
+        def scale_columns_on_vector(n, j):
+            if on_vector(n, j):
+                scale_quarter(n, j, nc.vector, 0)
+
         def scale_columns(n, j):
+            if not on_vector(n, j):
+                scale_quarter(n, j, nc.gpsimd, j)
+
+        def scale_quarter(n, j, engine, release):
             if j == 0:
                 attn_grouped[n] = attn_pool.tile([P, ENTRIES, PACK], BF16, name="attn_grouped", align_bytes=64)
                 attn_codes[n] = mx_pool.tile([P, ENTRIES], U32, name="attn_codes", align_bytes=64)
                 attn_scales[n] = mx_pool.tile([P, ENTRIES], U8, name="attn_scales", align_bytes=64)
             queries = slice(j * P, (j + 1) * P)
-            engine = nc.vector if n == POINTS - 1 and j in () else nc.gpsimd
             engine.tensor_tensor(
                 out=attn_grouped[n][:, queries, :].rearrange("p (b i) t -> p b t i", i=4),
                 in0=prob_t[n][:, :, queries].rearrange("p t (b i) -> p b t i", i=4),
-                in1=inv[PACK * n + j + COL - 1][:, 0:PACK].unsqueeze(1).unsqueeze(3).to_broadcast([P, P // 4, PACK, 4]),
+                in1=inv[PACK * n + release + COL - 1][:, 0:PACK].unsqueeze(1).unsqueeze(3).to_broadcast([P, P // 4, PACK, 4]),
                 op=ALU.mult,
             )
 
@@ -390,6 +400,7 @@ def tile_interral_pa_kernel(tc, xq, yk, y_feat, x_feat, W_v, b_v, out):
                 run(quantise_features, tick + FEAT_LEAD - 4)
                 run(quantise_values, tick - VQ)
                 run(quantise_attention, tick - AQ)
+                run(scale_columns_on_vector, tick - COL)
                 run(invert, tick - 1, QUARTERS + 4 * PACK)
                 run(build_diagonal, tick - 1)
                 run(sum_columns, tick - FLIP)

@@ -31,7 +31,7 @@ VQ = 11
 FLIP = 6
 COL = 10
 AQ = 14
-OUT = 14
+OUT = 15
 EARLY_P = 2
 EARLY_F = 2
 
@@ -48,7 +48,7 @@ def tile_interral_pa_kernel(tc, xq, yk, y_feat, x_feat, W_v, b_v, out):
         soft = ctx.enter_context(tc.tile_pool(name="soft", bufs=3))
         stats = ctx.enter_context(tc.tile_pool(name="stats", bufs=4))
         inv_pool = ctx.enter_context(tc.tile_pool(name="inv", bufs=8))
-        result_pool = ctx.enter_context(tc.tile_pool(name="result", bufs=4))
+        result_pool = ctx.enter_context(tc.tile_pool(name="result", bufs=8))
         psum_flip = ctx.enter_context(tc.psum_pool(name="psum_flip", bufs=4))
         psum_energy = ctx.enter_context(tc.psum_pool(name="psum_energy", bufs=2))
         psum_mx = ctx.enter_context(tc.psum_pool(name="psum_mx", bufs=2))
@@ -208,13 +208,16 @@ def tile_interral_pa_kernel(tc, xq, yk, y_feat, x_feat, W_v, b_v, out):
             n = (i + 1 - COL) // PACK
             if 0 <= n < POINTS:
                 first = 0
-                if (i + 1 - COL) % PACK == 0:
-                    nc.vector.tensor_scalar_add(out=stat[q][:, 0:PACK], in0=col_sum[n][:], scalar1=EPS_L1)
             if i < QUARTERS:
                 last = c + 1
             if last > first:
                 inv[i] = inv_pool.tile([P, 2 * PACK], F32, name="inv")
                 nc.vector.reciprocal(out=inv[i][:, first:last], in_=stat[q][:, first:last])
+
+        def add_epsilon(n, j):
+            if j == 0:
+                q, c = stat_of(PACK * n + COL - 1)
+                nc.vector.tensor_scalar_add(out=stat[q][:, 0:PACK], in0=col_sum[n][:], scalar1=EPS_L1)
 
         diagonal = {}
 
@@ -223,7 +226,7 @@ def tile_interral_pa_kernel(tc, xq, yk, y_feat, x_feat, W_v, b_v, out):
             if how == "D":
                 q, c = stat_of(PACK * n + j)
                 diagonal[n, j] = stats.tile([P, P], F32, name="diagonal", bufs=6)
-                nc.gpsimd.tensor_scalar(out=diagonal[n, j][:], in0=ident_f32[:], scalar1=inv[PACK * n + j][:, c : c + 1], scalar2=0.0, op0=ALU.mult, op1=ALU.add)
+                nc.scalar.activation(out=diagonal[n, j][:], in_=ident_f32[:], func=ACT.Copy, scale=inv[PACK * n + j][:, c : c + 1])
 
         def scale_rows(n, j):
             q, c = stat_of(PACK * n + j)
@@ -332,7 +335,7 @@ def tile_interral_pa_kernel(tc, xq, yk, y_feat, x_feat, W_v, b_v, out):
                 )
 
         def on_vector(n, j):
-            return j == 3
+            return j == 3 or n == 7 and j > 0
 
         def scale_columns_on_vector(n, j):
             if on_vector(n, j):
@@ -382,7 +385,7 @@ def tile_interral_pa_kernel(tc, xq, yk, y_feat, x_feat, W_v, b_v, out):
                 nc.vector.tensor_tensor(out=result[:], in0=x_sb[n][:, j, :], in1=yr_acc[n, j][:], op=ALU.subtract)
             nc.sync.dma_start(out=out_rows[n, j], in_=result[:])
 
-        ROW = {0: "S", 1: "S", 2: "S", 3: "S"}
+        ROW = {0: "S", 1: "D", 2: "S", 3: "S"}
         SUBG = ()
 
         def run(stage, index, count=QUARTERS):
@@ -396,31 +399,30 @@ def tile_interral_pa_kernel(tc, xq, yk, y_feat, x_feat, W_v, b_v, out):
         with tc.manual_schedule():
             for tick in range(-PROJ_LEAD - 1, QUARTERS + OUT):
                 run(row_max, tick)
+                run(add_epsilon, tick - COL)
                 run(quantise_weights, tick + WL - 2, PACK)
                 run(quantise_features, tick + FEAT_LEAD - 4)
                 run(quantise_values, tick - VQ)
                 run(quantise_attention, tick - AQ)
                 run(scale_columns_on_vector, tick - COL)
                 run(invert, tick - 1, QUARTERS + 4 * PACK)
-                run(build_diagonal, tick - 1)
+                run(build_diagonal, tick - 2)
+                run(scale_rows, tick - 2)
                 run(sum_columns, tick - FLIP)
                 run(exponentials, tick)
-                run(scale_rows, tick - 1)
                 run(scale_columns, tick - COL)
                 run(evacuate_projections, tick + PROJ_LEAD)
                 run(evacuate_weights, tick + WL, PACK)
                 run(evacuate_features, tick + FEAT_LEAD)
                 run(add_bias, tick - VALUES)
-                run(add_bias_turned, tick - VALUES)
                 run(evacuate_values, tick - VALUES - 2)
-                run(output_mx, tick - OUT)
+                run(add_bias_turned, tick - VALUES)
                 run(subtract_attended, tick - OUT)
                 run(energies, tick + 1)
-                run(flip_probabilities, tick + 1 - FLIP)
                 run(flip_values, tick - VALUES - 1)
                 run(prepare_projections, tick + PROJ_LEAD + 1)
                 run(prepare_weights, tick + WL + 1, PACK)
                 run(prepare_features, tick + FEAT_LEAD + 1)
-                if tick == -1:
-                    prepare_bias()
+                run(flip_probabilities, tick + 1 - FLIP)
                 run(values_mx, tick + 1 - VALUES)
+                run(output_mx, tick + 1 - OUT)

@@ -23,15 +23,16 @@ FLOPS = 2 * POINTS * ENTRIES * (CHANNELS * CHANNELS + ENTRIES * QK + ENTRIES * C
 
 
 QUARTERS = POINTS * PACK
+OFF = 1
 WL = -1
 PROJ_LEAD = 4
 FEAT_LEAD = 0
 VALUES = 5
-VQ = 11
+VQ = 9
 FLIP = 6
-COL = 10
-AQ = 14
-OUT = 15
+COL = 8
+AQ = 11
+OUT = 12
 EARLY_P = 2
 EARLY_F = 2
 
@@ -67,8 +68,15 @@ def tile_interral_pa_kernel(tc, xq, yk, y_feat, x_feat, W_v, b_v, out):
             yk_sb.append(resident.tile([P, PACK, QK], BF16, name="yk%d" % n))
             y_sb.append(resident.tile([P, PACK, CHANNELS], BF16, name="y%d" % n))
             x_sb.append(resident.tile([P, PACK, CHANNELS], BF16, name="x%d" % n))
+        def load_projections(n):
             nc.sync.dma_start(out=xq_sb[n][:], in_=xq_rows[n])
             nc.sync.dma_start(out=yk_sb[n][:], in_=yk_rows[n])
+
+        load_projections(0)
+        load_projections(1)
+        for n in range(POINTS):
+            if 0 < n < POINTS - 1:
+                load_projections(n + 1)
             if n == 0:
                 nc.sync.dma_start(out=w_sb[:], in_=W_v.rearrange("(i p) k -> p i k", p=P))
             nc.sync.dma_start(out=y_sb[n][:], in_=y_rows[n])
@@ -136,23 +144,23 @@ def tile_interral_pa_kernel(tc, xq, yk, y_feat, x_feat, W_v, b_v, out):
 
         def evacuate_projections(n, j):
             if j < 2:
-                copy = nc.vector.tensor_copy if n < 3 and (n, j) != (0, 0) else nc.scalar.copy
+                copy = nc.vector.tensor_copy if n < 3 and j == 1 else nc.scalar.copy
                 t = proj.tile([P, ENTRIES], BF16, name="proj%d" % j)
                 (xq_t, yk_t)[j][n] = t
                 copy(out=t[:], in_=flipped["p", n, j][:].rearrange("d g r -> d (g r)"))
 
         def prepare_features(n, j):
-            if j >= 2:
-                channels_to_partitions(y_sb[n], ("y", n, j), j - 2)
+            if j < 2:
+                channels_to_partitions(y_sb[n], ("y", n, j), j)
 
         def evacuate_features(n, j):
-            if j == 2:
+            if j == 0:
                 y_grouped[n] = grouped_pool.tile([P, ENTRIES, PACK], BF16, name="y_grouped", align_bytes=64)
                 y_codes[n] = mx_pool.tile([P, ENTRIES], U32, name="y_codes", align_bytes=64)
                 y_scales[n] = mx_pool.tile([P, ENTRIES], U8, name="y_scales", align_bytes=64)
-            if j >= 2:
-                copy = nc.vector.tensor_copy if n < 3 else nc.scalar.copy
-                evacuate_channels(("y", n, j), y_grouped[n], j - 2, copy)
+            if j < 2:
+                copy = nc.vector.tensor_copy if 0 < n < 3 else nc.scalar.copy
+                evacuate_channels(("y", n, j), y_grouped[n], j, copy)
 
         def quantise_features(n, j):
             if j == 0:
@@ -185,10 +193,10 @@ def tile_interral_pa_kernel(tc, xq, yk, y_feat, x_feat, W_v, b_v, out):
             )
 
         def stat_of(i):
-            q = (i + 3) // PACK
+            q = (i + OFF) // PACK
             if q not in stat:
                 stat[q] = stats.tile([P, 2 * PACK], F32, name="stat")
-            return q, PACK + (i + 3) % PACK
+            return q, PACK + (i + OFF) % PACK
 
         def exponentials(n, j):
             q, c = stat_of(PACK * n + j)
@@ -204,7 +212,7 @@ def tile_interral_pa_kernel(tc, xq, yk, y_feat, x_feat, W_v, b_v, out):
         def invert(m, j):
             i = PACK * m + j
             q, c = stat_of(i)
-            first, last = (PACK if i > 0 else 2 * PACK - 1), PACK
+            first, last = PACK + (OFF if i + OFF < PACK else 0), PACK
             n = (i + 1 - COL) // PACK
             if 0 <= n < POINTS:
                 first = 0
@@ -334,19 +342,23 @@ def tile_interral_pa_kernel(tc, xq, yk, y_feat, x_feat, W_v, b_v, out):
                     out=prob_t[n][:, t, :], in_=flipped_prob[n, t][:], func=ACT.Copy, accum_out=col_sum[n][:, t : t + 1]
                 )
 
-        def on_vector(n, j):
-            return j == 3 or n == 7 and j > 0
+        def scale_columns_on_vector(n, k):
+            if n < POINTS - 1 and k == 2:
+                scale_quarter(n, 3, nc.vector, 0)
+            if n == POINTS - 1 and k == 1:
+                scale_quarter(n, 2, nc.vector, 0)
+                scale_quarter(n, 3, nc.vector, 0)
 
-        def scale_columns_on_vector(n, j):
-            if on_vector(n, j):
-                scale_quarter(n, j, nc.vector, 0)
+        def scale_columns_behind(n, k):
+            if n == POINTS - 1 and k == 0:
+                scale_quarter(n, 1, nc.vector, 0)
 
-        def scale_columns(n, j):
-            if not on_vector(n, j):
-                scale_quarter(n, j, nc.gpsimd, j)
+        def scale_columns(n, k):
+            if k == 0 or n < POINTS - 1 and k < 3:
+                scale_quarter(n, k, nc.gpsimd, k)
 
         def scale_quarter(n, j, engine, release):
-            if j == 0:
+            if n not in attn_grouped:
                 attn_grouped[n] = attn_pool.tile([P, ENTRIES, PACK], BF16, name="attn_grouped", align_bytes=64)
                 attn_codes[n] = mx_pool.tile([P, ENTRIES], U32, name="attn_codes", align_bytes=64)
                 attn_scales[n] = mx_pool.tile([P, ENTRIES], U8, name="attn_scales", align_bytes=64)
@@ -364,7 +376,10 @@ def tile_interral_pa_kernel(tc, xq, yk, y_feat, x_feat, W_v, b_v, out):
 
         def output_mx(n, j):
             queries = slice(j * P, (j + 1) * P)
-            yr_acc[n, j] = psum_mx.tile([P, CHANNELS], F32, name="yr_acc", tag="acc")
+            if n == POINTS - 1 and j % 2 == 1:
+                yr_acc[n, j] = psum_energy.tile([P, CHANNELS], F32, name="energy")
+            else:
+                yr_acc[n, j] = psum_mx.tile([P, CHANNELS], F32, name="yr_acc", tag="acc")
             nc.tensor.matmul_mx(
                 out=yr_acc[n, j][:],
                 lhsT=attn_codes[n][:, queries].bitcast(FP8X4),
@@ -385,12 +400,17 @@ def tile_interral_pa_kernel(tc, xq, yk, y_feat, x_feat, W_v, b_v, out):
                 nc.vector.tensor_tensor(out=result[:], in0=x_sb[n][:, j, :], in1=yr_acc[n, j][:], op=ALU.subtract)
             nc.sync.dma_start(out=out_rows[n, j], in_=result[:])
 
-        ROW = {0: "S", 1: "D", 2: "S", 3: "S"}
+        ROW = {0: "S", 1: "S", 2: "S", 3: "D"}
         SUBG = ()
 
         def run(stage, index, count=QUARTERS):
             if 0 <= index < count:
                 stage(index // PACK, index % PACK)
+
+        def run_pairs(stage, index):
+            if 0 <= index < QUARTERS and index % PACK < 2:
+                for t in (2 * (index % PACK), 2 * (index % PACK) + 1):
+                    stage(index // PACK, t)
 
         w_grouped = resident.tile([P, CHANNELS, PACK], BF16, align_bytes=64)
         w_codes = resident.tile([P, CHANNELS], U32, align_bytes=64)
@@ -401,28 +421,27 @@ def tile_interral_pa_kernel(tc, xq, yk, y_feat, x_feat, W_v, b_v, out):
                 run(row_max, tick)
                 run(add_epsilon, tick - COL)
                 run(quantise_weights, tick + WL - 2, PACK)
-                run(quantise_features, tick + FEAT_LEAD - 4)
+                run(quantise_features, tick - 4)
                 run(quantise_values, tick - VQ)
-                run(quantise_attention, tick - AQ)
                 run(scale_columns_on_vector, tick - COL)
                 run(invert, tick - 1, QUARTERS + 4 * PACK)
+                run(scale_columns_behind, tick - COL)
+                run(add_bias_turned, tick - VALUES)
                 run(build_diagonal, tick - 2)
                 run(scale_rows, tick - 2)
-                run(sum_columns, tick - FLIP)
+                run_pairs(sum_columns, tick - FLIP)
                 run(exponentials, tick)
                 run(scale_columns, tick - COL)
                 run(evacuate_projections, tick + PROJ_LEAD)
                 run(evacuate_weights, tick + WL, PACK)
                 run(evacuate_features, tick + FEAT_LEAD)
                 run(add_bias, tick - VALUES)
-                run(evacuate_values, tick - VALUES - 2)
-                run(add_bias_turned, tick - VALUES)
+                run(quantise_attention, tick - AQ)
                 run(subtract_attended, tick - OUT)
                 run(energies, tick + 1)
-                run(flip_values, tick - VALUES - 1)
                 run(prepare_projections, tick + PROJ_LEAD + 1)
                 run(prepare_weights, tick + WL + 1, PACK)
                 run(prepare_features, tick + FEAT_LEAD + 1)
-                run(flip_probabilities, tick + 1 - FLIP)
+                run_pairs(flip_probabilities, tick + 1 - FLIP)
                 run(values_mx, tick + 1 - VALUES)
                 run(output_mx, tick + 1 - OUT)

@@ -28,11 +28,11 @@ WL = -1
 PROJ_LEAD = 4
 FEAT_LEAD = 0
 VALUES = 5
-VQ = 9
+VQ = 11
 FLIP = 6
 COL = 8
-AQ = 11
-OUT = 12
+AQ = 13
+OUT = 14
 EARLY_P = 2
 EARLY_F = 2
 
@@ -77,9 +77,9 @@ def tile_interral_pa_kernel(tc, xq, yk, y_feat, x_feat, W_v, b_v, out):
         for n in range(POINTS):
             if 0 < n < POINTS - 1:
                 load_projections(n + 1)
+            nc.sync.dma_start(out=y_sb[n][:], in_=y_rows[n])
             if n == 0:
                 nc.sync.dma_start(out=w_sb[:], in_=W_v.rearrange("(i p) k -> p i k", p=P))
-            nc.sync.dma_start(out=y_sb[n][:], in_=y_rows[n])
             if n == 0:
                 nc.sync.dma_start(out=bias_sb[:], in_=b_v.partition_broadcast(P))
             elif n > 1:
@@ -343,8 +343,6 @@ def tile_interral_pa_kernel(tc, xq, yk, y_feat, x_feat, W_v, b_v, out):
                 )
 
         def scale_columns_on_vector(n, k):
-            if n < POINTS - 1 and k == 2:
-                scale_quarter(n, 3, nc.vector, 0)
             if n == POINTS - 1 and k == 1:
                 scale_quarter(n, 2, nc.vector, 0)
                 scale_quarter(n, 3, nc.vector, 0)
@@ -354,7 +352,7 @@ def tile_interral_pa_kernel(tc, xq, yk, y_feat, x_feat, W_v, b_v, out):
                 scale_quarter(n, 1, nc.vector, 0)
 
         def scale_columns(n, k):
-            if k == 0 or n < POINTS - 1 and k < 3:
+            if k == 0 or n < POINTS - 1:
                 scale_quarter(n, k, nc.gpsimd, k)
 
         def scale_quarter(n, j, engine, release):
@@ -400,7 +398,7 @@ def tile_interral_pa_kernel(tc, xq, yk, y_feat, x_feat, W_v, b_v, out):
                 nc.vector.tensor_tensor(out=result[:], in0=x_sb[n][:, j, :], in1=yr_acc[n, j][:], op=ALU.subtract)
             nc.sync.dma_start(out=out_rows[n, j], in_=result[:])
 
-        ROW = {0: "S", 1: "S", 2: "S", 3: "D"}
+        ROW = {0: "D", 1: "S", 2: "S", 3: "S"}
         SUBG = ()
 
         def run(stage, index, count=QUARTERS):
@@ -423,6 +421,7 @@ def tile_interral_pa_kernel(tc, xq, yk, y_feat, x_feat, W_v, b_v, out):
                 run(quantise_weights, tick + WL - 2, PACK)
                 run(quantise_features, tick - 4)
                 run(quantise_values, tick - VQ)
+                run(quantise_attention, tick - AQ)
                 run(scale_columns_on_vector, tick - COL)
                 run(invert, tick - 1, QUARTERS + 4 * PACK)
                 run(scale_columns_behind, tick - COL)
@@ -436,9 +435,11 @@ def tile_interral_pa_kernel(tc, xq, yk, y_feat, x_feat, W_v, b_v, out):
                 run(evacuate_weights, tick + WL, PACK)
                 run(evacuate_features, tick + FEAT_LEAD)
                 run(add_bias, tick - VALUES)
-                run(quantise_attention, tick - AQ)
                 run(subtract_attended, tick - OUT)
-                run(energies, tick + 1)
+                if tick != 0:
+                    run(energies, tick + 1)
+                if tick == -1:
+                    run(energies, 1)
                 run(prepare_projections, tick + PROJ_LEAD + 1)
                 run(prepare_weights, tick + WL + 1, PACK)
                 run(prepare_features, tick + FEAT_LEAD + 1)

@@ -417,21 +417,21 @@ def tile_interral_pa_kernel(tc, xq, yk, y_feat, x_feat, W_v, b_v, out):
         with tc.manual_schedule():
             for tick in range(-PROJ_LEAD - 1, QUARTERS + OUT):
                 run(row_max, tick)
+                run(evacuate_projections, tick + PROJ_LEAD)
                 run(add_epsilon, tick - COL)
                 run(quantise_weights, tick + WL - 2, PACK)
                 run(quantise_features, tick - 4)
-                run(quantise_values, tick - VQ)
                 run(quantise_attention, tick - AQ)
                 run(scale_columns_on_vector, tick - COL)
                 run(invert, tick - 1, QUARTERS + 4 * PACK)
                 run(scale_columns_behind, tick - COL)
+                run(quantise_values, tick - VQ)
                 run(add_bias_turned, tick - VALUES)
                 run(build_diagonal, tick - 2)
                 run(scale_rows, tick - 2)
                 run_pairs(sum_columns, tick - FLIP)
                 run(exponentials, tick)
                 run(scale_columns, tick - COL)
-                run(evacuate_projections, tick + PROJ_LEAD)
                 run(evacuate_weights, tick + WL, PACK)
                 run(evacuate_features, tick + FEAT_LEAD)
                 run(add_bias, tick - VALUES)

@@ -14,27 +14,31 @@ ACT = mybir.ActivationFunctionType
 P = 128
 PACK = 4
 POINTS = 8
+LAST = POINTS - 1
 ENTRIES = 512
 CHANNELS = 512
 QK = 128
 EPS_L1 = 1e-9
+RUN = 4
 
 FLOPS = 2 * POINTS * ENTRIES * (CHANNELS * CHANNELS + ENTRIES * QK + ENTRIES * CHANNELS)
 
-
 QUARTERS = POINTS * PACK
-OFF = 1
-WL = -1
-PROJ_LEAD = 4
-FEAT_LEAD = 0
-VALUES = 5
-VQ = 11
-FLIP = 6
-COL = 8
-AQ = 13
-OUT = 14
-EARLY_P = 2
-EARLY_F = 2
+PROJECTIONS_LEAD = 4
+WEIGHTS_DELAY = 1
+WEIGHTS_QUANTISE_DELAY = 3
+FEATURES_QUANTISE_DELAY = 4
+VALUES_DELAY = 5
+ROWS_DELAY = 2
+TURN_DELAY = 6
+COLUMNS_DELAY = 8
+VALUES_QUANTISE_DELAY = 11
+ATTENTION_QUANTISE_DELAY = 13
+OUTPUT_DELAY = 14
+
+DIAGONAL_QUARTER = 0
+KEYS_ON_VECTOR = (0, 1, 2)
+FEATURES_ON_VECTOR = (1, 2)
 
 
 def tile_interral_pa_kernel(tc, xq, yk, y_feat, x_feat, W_v, b_v, out):
@@ -43,14 +47,14 @@ def tile_interral_pa_kernel(tc, xq, yk, y_feat, x_feat, W_v, b_v, out):
         resident = ctx.enter_context(tc.tile_pool(name="resident", bufs=1))
         proj = ctx.enter_context(tc.tile_pool(name="proj", bufs=3))
         grouped_pool = ctx.enter_context(tc.tile_pool(name="grouped", bufs=2))
-        attn_pool = ctx.enter_context(tc.tile_pool(name="attn", bufs=2))
         mx_pool = ctx.enter_context(tc.tile_pool(name="mx", bufs=2))
         values_pool = ctx.enter_context(tc.tile_pool(name="values", bufs=5))
         soft = ctx.enter_context(tc.tile_pool(name="soft", bufs=3))
         stats = ctx.enter_context(tc.tile_pool(name="stats", bufs=4))
-        inv_pool = ctx.enter_context(tc.tile_pool(name="inv", bufs=8))
+        inverse_pool = ctx.enter_context(tc.tile_pool(name="inverse", bufs=8))
+        diagonal_pool = ctx.enter_context(tc.tile_pool(name="diagonal", bufs=6))
         result_pool = ctx.enter_context(tc.tile_pool(name="result", bufs=8))
-        psum_flip = ctx.enter_context(tc.psum_pool(name="psum_flip", bufs=4))
+        psum_turn = ctx.enter_context(tc.psum_pool(name="psum_turn", bufs=4))
         psum_energy = ctx.enter_context(tc.psum_pool(name="psum_energy", bufs=2))
         psum_mx = ctx.enter_context(tc.psum_pool(name="psum_mx", bufs=2))
 
@@ -68,6 +72,7 @@ def tile_interral_pa_kernel(tc, xq, yk, y_feat, x_feat, W_v, b_v, out):
             yk_sb.append(resident.tile([P, PACK, QK], BF16, name="yk%d" % n))
             y_sb.append(resident.tile([P, PACK, CHANNELS], BF16, name="y%d" % n))
             x_sb.append(resident.tile([P, PACK, CHANNELS], BF16, name="x%d" % n))
+
         def load_projections(n):
             nc.sync.dma_start(out=xq_sb[n][:], in_=xq_rows[n])
             nc.sync.dma_start(out=yk_sb[n][:], in_=yk_rows[n])
@@ -75,16 +80,15 @@ def tile_interral_pa_kernel(tc, xq, yk, y_feat, x_feat, W_v, b_v, out):
         load_projections(0)
         load_projections(1)
         for n in range(POINTS):
-            if 0 < n < POINTS - 1:
+            if 0 < n < LAST:
                 load_projections(n + 1)
             nc.sync.dma_start(out=y_sb[n][:], in_=y_rows[n])
             if n == 0:
                 nc.sync.dma_start(out=w_sb[:], in_=W_v.rearrange("(i p) k -> p i k", p=P))
-            if n == 0:
                 nc.sync.dma_start(out=bias_sb[:], in_=b_v.partition_broadcast(P))
             elif n > 1:
                 nc.sync.dma_start(out=x_sb[n - 2][:], in_=x_rows[n - 2])
-        for n in (POINTS - 2, POINTS - 1):
+        for n in (LAST - 1, LAST):
             nc.sync.dma_start(out=x_sb[n][:], in_=x_rows[n])
 
         ident_f32 = resident.tile([P, P], F32)
@@ -92,66 +96,53 @@ def tile_interral_pa_kernel(tc, xq, yk, y_feat, x_feat, W_v, b_v, out):
         ident_bf16 = resident.tile([P, P], BF16)
         make_identity(nc, ident_bf16[:])
 
+        w_grouped = resident.tile([P, CHANNELS, PACK], BF16, align_bytes=64)
+        w_codes = resident.tile([P, CHANNELS], U32, align_bytes=64)
+        w_scales = resident.tile([P, CHANNELS], U8, align_bytes=64)
+
+        turned_w, turned_y, turned_proj, turned_p = {}, {}, {}, {}
         y_grouped, y_codes, y_scales = {}, {}, {}
         xq_t, yk_t = {}, {}
-        energy = {}
-        neg_max, stat, inv, prob = {}, {}, {}, {}
-        yv_grouped, yv_codes, yv_scales = {}, {}, {}
-        yv_acc, yr_acc = {}, {}
+        energy, neg_max, prob = {}, {}, {}
+        sums, inverses, diagonal = {}, {}, {}
+        yv_acc, yv_grouped, yv_codes, yv_scales = {}, {}, {}, {}
         col_sum, prob_t = {}, {}
-        attn_grouped, attn_codes, attn_scales = {}, {}, {}
+        attn_grouped, attn_codes, attn_scales, yr_acc = {}, {}, {}, {}
 
-        bias_column = resident.tile([P, PACK], F32)
-
-        def prepare_bias():
-            turned = psum_flip.tile([P, PACK, P], BF16, name="flipped_p", tag="flip")
-            for c in range(PACK):
-                nc.tensor.transpose(turned[:, c, :], bias_sb[:, c * P : (c + 1) * P], ident_bf16[:])
-            nc.vector.tensor_copy(out=bias_column[:], in_=turned[:, :, 0])
-
-        def quantise(codes, scales, grouped, first, count):
-            cols = slice(first, first + count)
+        def quantise(codes, scales, grouped):
             nc.vector.quantize_mx(
-                out=codes[:, cols].bitcast(FP8X4),
-                scales=scales[:, cols],
-                in_=grouped[:, cols, :].rearrange("q r t -> q (r t)"),
+                out=codes[:].bitcast(FP8X4), scales=scales[:], in_=grouped[:].rearrange("q r t -> q (r t)")
             )
 
-        flipped = {}
-
-        def channels_to_partitions(rows_sb, key, pair):
+        def turn_channels(rows_sb, pair):
             words = rows_sb[:].bitcast(F32)
-            flipped[key] = psum_flip.tile([P, 2, 2, P], F32, name="flipped", tag="flip")
+            turned = psum_turn.tile([P, 2, 2, P], F32, name="turned_channels", tag="turn")
             for g in range(2):
                 for u in range(2):
                     nc.tensor.transpose(
-                        flipped[key][:, g, u, :], words[:, 2 * pair + g, u * P : (u + 1) * P], ident_f32[:]
+                        turned[:, g, u, :], words[:, 2 * pair + g, u * P : (u + 1) * P], ident_f32[:]
                     )
+            return turned
 
-        def evacuate_channels(key, grouped, pair, copy):
-            grouped_words = grouped[:].bitcast(F32).rearrange("q (g r) u -> q g r u", g=PACK)
-            copy(
-                out=grouped_words[:, 2 * pair : 2 * pair + 2],
-                in_=flipped[key][:].rearrange("q g u r -> q g r u"),
-            )
+        def evacuate_channels(turned, grouped, pair, copy):
+            words = grouped[:].bitcast(F32).rearrange("q (g r) u -> q g r u", g=PACK)
+            copy(out=words[:, 2 * pair : 2 * pair + 2], in_=turned[:].rearrange("q g u r -> q g r u"))
 
-        def prepare_projections(n, j):
+        def turn_weights(j):
             if j < 2:
-                rows_sb = (xq_sb, yk_sb)[j][n]
-                flipped["p", n, j] = psum_flip.tile([P, PACK, P], BF16, name="flipped_p", tag="flip")
-                for g in range(PACK):
-                    nc.tensor.transpose(flipped["p", n, j][:, g, :], rows_sb[:, g, :], ident_bf16[:])
+                turned_w[j] = turn_channels(w_sb, j)
 
-        def evacuate_projections(n, j):
+        def evacuate_weights(j):
             if j < 2:
-                copy = nc.vector.tensor_copy if n < 3 and j == 1 else nc.scalar.copy
-                t = proj.tile([P, ENTRIES], BF16, name="proj%d" % j)
-                (xq_t, yk_t)[j][n] = t
-                copy(out=t[:], in_=flipped["p", n, j][:].rearrange("d g r -> d (g r)"))
+                evacuate_channels(turned_w[j], w_grouped, j, nc.vector.tensor_copy)
 
-        def prepare_features(n, j):
+        def quantise_weights(j):
+            if j == 0:
+                quantise(w_codes, w_scales, w_grouped)
+
+        def turn_features(n, j):
             if j < 2:
-                channels_to_partitions(y_sb[n], ("y", n, j), j)
+                turned_y[n, j] = turn_channels(y_sb[n], j)
 
         def evacuate_features(n, j):
             if j == 0:
@@ -159,112 +150,37 @@ def tile_interral_pa_kernel(tc, xq, yk, y_feat, x_feat, W_v, b_v, out):
                 y_codes[n] = mx_pool.tile([P, ENTRIES], U32, name="y_codes", align_bytes=64)
                 y_scales[n] = mx_pool.tile([P, ENTRIES], U8, name="y_scales", align_bytes=64)
             if j < 2:
-                copy = nc.vector.tensor_copy if 0 < n < 3 else nc.scalar.copy
-                evacuate_channels(("y", n, j), y_grouped[n], j, copy)
+                copy = nc.vector.tensor_copy if n in FEATURES_ON_VECTOR else nc.scalar.copy
+                evacuate_channels(turned_y[n, j], y_grouped[n], j, copy)
 
         def quantise_features(n, j):
             if j == 0:
-                quantise(y_codes[n], y_scales[n], y_grouped[n], 0, ENTRIES)
+                quantise(y_codes[n], y_scales[n], y_grouped[n])
 
-        def prepare_weights(n, j):
+        def turn_projections(n, j):
             if j < 2:
-                channels_to_partitions(w_sb, ("w", j), j)
+                rows_sb = (xq_sb, yk_sb)[j][n]
+                turned_proj[n, j] = psum_turn.tile([P, PACK, P], BF16, name="turned_proj", tag="turn")
+                for g in range(PACK):
+                    nc.tensor.transpose(turned_proj[n, j][:, g, :], rows_sb[:, g, :], ident_bf16[:])
 
-        def evacuate_weights(n, j):
+        def evacuate_projections(n, j):
             if j < 2:
-                evacuate_channels(("w", j), w_grouped, j, nc.vector.tensor_copy if True else nc.scalar.copy)
+                copy = nc.vector.tensor_copy if j == 1 and n in KEYS_ON_VECTOR else nc.scalar.copy
+                columns = proj.tile([P, ENTRIES], BF16, name=("xq_t", "yk_t")[j])
+                (xq_t, yk_t)[j][n] = columns
+                copy(out=columns[:], in_=turned_proj[n, j][:].rearrange("d g r -> d (g r)"))
 
-        def quantise_weights(n, j):
-            if j == 0:
-                quantise(w_codes, w_scales, w_grouped, 0, CHANNELS)
-
-        def energies(n, j):
-            energy[n, j] = psum_energy.tile([P, ENTRIES], F32, name="energy")
-            nc.tensor.matmul(
-                out=energy[n, j][:], lhsT=xq_t[n][:, j * P : (j + 1) * P], rhs=yk_t[n][:], start=True, stop=True
-            )
-
-        def row_max(n, j):
-            if j == 0:
-                neg_max[n] = stats.tile([P, PACK], F32, name="neg_max")
-                prob[n] = soft.tile([P, PACK, ENTRIES], F32, name="prob")
-            nc.vector.tensor_reduce(
-                out=neg_max[n][:, j : j + 1], in_=energy[n, j][:], axis=mybir.AxisListType.X, op=ALU.max, negate=True
-            )
-
-        def stat_of(i):
-            q = (i + OFF) // PACK
-            if q not in stat:
-                stat[q] = stats.tile([P, 2 * PACK], F32, name="stat")
-            return q, PACK + (i + OFF) % PACK
-
-        def exponentials(n, j):
-            q, c = stat_of(PACK * n + j)
-            nc.scalar.activation(
-                out=prob[n][:, j, :],
-                in_=energy[n, j][:],
-                func=ACT.Exp,
-                bias=neg_max[n][:, j : j + 1],
-                scale=1.0,
-                accum_out=stat[q][:, c : c + 1],
-            )
-
-        def invert(m, j):
-            i = PACK * m + j
-            q, c = stat_of(i)
-            first, last = PACK + (OFF if i + OFF < PACK else 0), PACK
-            n = (i + 1 - COL) // PACK
-            if 0 <= n < POINTS:
-                first = 0
-            if i < QUARTERS:
-                last = c + 1
-            if last > first:
-                inv[i] = inv_pool.tile([P, 2 * PACK], F32, name="inv")
-                nc.vector.reciprocal(out=inv[i][:, first:last], in_=stat[q][:, first:last])
-
-        def add_epsilon(n, j):
-            if j == 0:
-                q, c = stat_of(PACK * n + COL - 1)
-                nc.vector.tensor_scalar_add(out=stat[q][:, 0:PACK], in0=col_sum[n][:], scalar1=EPS_L1)
-
-        diagonal = {}
-
-        def build_diagonal(n, j):
-            how = ROW[(n, j)] if (n, j) in ROW else ROW[j]
-            if how == "D":
-                q, c = stat_of(PACK * n + j)
-                diagonal[n, j] = stats.tile([P, P], F32, name="diagonal", bufs=6)
-                nc.scalar.activation(out=diagonal[n, j][:], in_=ident_f32[:], func=ACT.Copy, scale=inv[PACK * n + j][:, c : c + 1])
-
-        def scale_rows(n, j):
-            q, c = stat_of(PACK * n + j)
-            scale = inv[PACK * n + j][:, c : c + 1]
-            how = ROW[(n, j)] if (n, j) in ROW else ROW[j]
-            if how == "S":
-                nc.scalar.activation(out=prob[n][:, j, :], in_=prob[n][:, j, :], func=ACT.Copy, scale=scale)
-            elif how == "V":
-                nc.vector.tensor_scalar_mul(out=prob[n][:, j, :], in0=prob[n][:, j, :], scalar1=scale)
-            elif how == "G":
-                nc.gpsimd.tensor_scalar(out=prob[n][:, j, :], in0=prob[n][:, j, :], scalar1=scale, scalar2=0.0, op0=ALU.mult, op1=ALU.add)
-
-        def values_mx(n, c):
+        def project_values(n, c):
             if c == 0:
                 yv_grouped[n] = grouped_pool.tile([P, CHANNELS, PACK], BF16, name="yv_grouped", align_bytes=64)
                 yv_codes[n] = values_pool.tile([P, CHANNELS], U32, name="yv_codes", align_bytes=64)
                 yv_scales[n] = values_pool.tile([P, CHANNELS], U8, name="yv_scales", align_bytes=64)
+            if n == LAST:
+                yv_acc[n, c] = psum_energy.tile([P, PACK, P], F32, name="late_values", tag="energy")
+            else:
+                yv_acc[n, c] = psum_mx.tile([P, PACK, P], F32, name="yv_acc", tag="acc")
             cols = slice(c * P, (c + 1) * P)
-            yv_acc[n, c] = psum_mx.tile([P, PACK, P], F32, name="yv_acc", tag="acc")
-            if False:
-                nc.tensor.matmul_mx(
-                    out=yv_acc[n, c][:].rearrange("p t c -> p (t c)"),
-                    lhsT=w_codes[:, cols].bitcast(FP8X4),
-                    lhsT_scale=w_scales[:, cols],
-                    rhs=y_codes[n][:].bitcast(FP8X4),
-                    rhs_scale=y_scales[n][:],
-                    start=True,
-                    stop=True,
-                )
-                return
             for t in range(PACK):
                 keys = slice(t * P, (t + 1) * P)
                 nc.tensor.matmul_mx(
@@ -277,36 +193,7 @@ def tile_interral_pa_kernel(tc, xq, yk, y_feat, x_feat, W_v, b_v, out):
                     stop=True,
                 )
 
-        yv_turned, yv_words = {}, {}
-
-        def add_bias_turned(n, c):
-            if False:
-                yv_turned[n, c] = soft.tile([P, 2, P, 2], BF16, name="yv_turned", bufs=2)
-                nc.scalar.activation(
-                    out=yv_turned[n, c][:],
-                    in_=yv_acc[n, c][:].rearrange("c (u e) p -> c u p e", u=2),
-                    func=ACT.Identity,
-                    bias=bias_column[:, c : c + 1],
-                    scale=1.0,
-                )
-
-        def flip_values(n, c):
-            if False:
-                words = yv_turned[n, c][:].rearrange("c u p e -> c (u p e)").bitcast(F32)
-                yv_words[n, c] = psum_flip.tile([P, 2, P], F32, name="yv_words", tag="flip")
-                for u in range(2):
-                    nc.tensor.transpose(yv_words[n, c][:, u, :], words[:, u * P : (u + 1) * P], ident_f32[:])
-
-        def evacuate_values(n, c):
-            if False:
-                grouped_words = yv_grouped[n][:].bitcast(F32)
-                nc.scalar.copy(
-                    out=grouped_words[:, c * P : (c + 1) * P, :], in_=yv_words[n, c][:].rearrange("p u c -> p c u")
-                )
-
         def add_bias(n, c):
-            if False:
-                return
             cols = slice(c * P, (c + 1) * P)
             nc.vector.tensor_tensor(
                 out=yv_grouped[n][:, cols, :],
@@ -317,67 +204,124 @@ def tile_interral_pa_kernel(tc, xq, yk, y_feat, x_feat, W_v, b_v, out):
 
         def quantise_values(n, j):
             if j == 0:
-                quantise(yv_codes[n], yv_scales[n], yv_grouped[n], 0, CHANNELS)
+                quantise(yv_codes[n], yv_scales[n], yv_grouped[n])
 
-        flipped_prob = {}
+        def multiply_energies(n, j):
+            if n == 0 and j > 1:
+                energy[n, j] = psum_mx.tile([P, ENTRIES], F32, name="early_energy", tag="acc")
+            else:
+                energy[n, j] = psum_energy.tile([P, ENTRIES], F32, name="energy", tag="energy")
+            nc.tensor.matmul(
+                out=energy[n, j][:], lhsT=xq_t[n][:, j * P : (j + 1) * P], rhs=yk_t[n][:], start=True, stop=True
+            )
 
-        def flip_probabilities(n, t):
+        def find_row_max(n, j):
+            if j == 0:
+                neg_max[n] = stats.tile([P, PACK], F32, name="neg_max")
+                prob[n] = soft.tile([P, PACK, ENTRIES], F32, name="prob")
+            nc.vector.tensor_reduce(
+                out=neg_max[n][:, j : j + 1], in_=energy[n, j][:], axis=mybir.AxisListType.X, op=ALU.max, negate=True
+            )
+
+        def sums_of(index):
+            shifted = index + (1 - COLUMNS_DELAY) % PACK
+            if shifted // PACK not in sums:
+                sums[shifted // PACK] = stats.tile([P, 2 * PACK], F32, name="sums")
+            return sums[shifted // PACK], PACK + shifted % PACK
+
+        def exponentiate(n, j):
+            tile, column = sums_of(PACK * n + j)
+            nc.scalar.activation(
+                out=prob[n][:, j, :],
+                in_=energy[n, j][:],
+                func=ACT.Exp,
+                bias=neg_max[n][:, j : j + 1],
+                scale=1.0,
+                accum_out=tile[:, column : column + 1],
+            )
+
+        def add_epsilon(n, j):
+            if j == 0:
+                tile = sums_of(PACK * n + COLUMNS_DELAY - 1)[0]
+                nc.vector.tensor_scalar_add(out=tile[:, 0:PACK], in0=col_sum[n][:], scalar1=EPS_L1)
+
+        def invert_sums(index):
+            tile, column = sums_of(index)
+            n, j = (index + 1 - COLUMNS_DELAY) // PACK, (index + 1 - COLUMNS_DELAY) % PACK
+            has_columns = 0 <= n < POINTS
+            first_row = PACK + (1 - COLUMNS_DELAY) % PACK if tile is sums_of(0)[0] else PACK
+            first = 0 if has_columns else first_row
+            last = column + 1 if index < QUARTERS else PACK
+            if n == LAST and j > 0:
+                return
+            inverses[index] = inverse_pool.tile([P, 2 * PACK], F32, name="inverses")
+            nc.vector.reciprocal(out=inverses[index][:, first:last], in_=tile[:, first:last])
+
+        def scale_rows(n, j):
+            index = PACK * n + j
+            column = sums_of(index)[1]
+            inverse = inverses[index][:, column : column + 1]
+            if j == DIAGONAL_QUARTER:
+                diagonal[n] = diagonal_pool.tile([P, P], F32, name="diagonal")
+                nc.scalar.activation(out=diagonal[n][:], in_=ident_f32[:], func=ACT.Copy, scale=inverse)
+            else:
+                nc.scalar.activation(out=prob[n][:, j, :], in_=prob[n][:, j, :], func=ACT.Copy, scale=inverse)
+
+        def turn_probabilities(n, t):
             if t == 0:
                 col_sum[n] = stats.tile([P, PACK], F32, name="col_sum")
-                prob_t[n] = soft.tile([P, PACK, ENTRIES], F32, name="prob_t", bufs=3)
-            flipped_prob[n, t] = psum_flip.tile([P, ENTRIES], F32, name="flipped_prob", tag="flip")
+                prob_t[n] = soft.tile([P, PACK, ENTRIES], F32, name="prob_t")
+            turned_p[n, t] = psum_turn.tile([P, ENTRIES], F32, name="turned_p", tag="turn")
             for j in range(PACK):
-                target = flipped_prob[n, t][:, j * P : (j + 1) * P]
+                target = turned_p[n, t][:, j * P : (j + 1) * P]
                 source = prob[n][:, j, t * P : (t + 1) * P]
-                if (n, j) in diagonal:
-                    nc.tensor.matmul(out=target, lhsT=source, rhs=diagonal[n, j][:], start=True, stop=True)
+                if j == DIAGONAL_QUARTER:
+                    nc.tensor.matmul(out=target, lhsT=source, rhs=diagonal[n][:], start=True, stop=True)
                 else:
                     nc.tensor.transpose(target, source, ident_f32[:])
 
         def sum_columns(n, t):
-            if n == POINTS - 1 and t % 2 == 1 and 0:
-                nc.vector.tensor_scalar(out=prob_t[n][:, t, :], in0=flipped_prob[n, t][:], scalar1=1.0, scalar2=None, op0=ALU.mult, op1=ALU.add, accum_out=col_sum[n][:, t : t + 1])
-            else:
-                nc.scalar.activation(
-                    out=prob_t[n][:, t, :], in_=flipped_prob[n, t][:], func=ACT.Copy, accum_out=col_sum[n][:, t : t + 1]
-                )
+            nc.scalar.activation(
+                out=prob_t[n][:, t, :], in_=turned_p[n, t][:], func=ACT.Copy, accum_out=col_sum[n][:, t : t + 1]
+            )
 
-        def scale_columns_on_vector(n, k):
-            if n == POINTS - 1 and k == 1:
-                scale_quarter(n, 2, nc.vector, 0)
-                scale_quarter(n, 3, nc.vector, 0)
-
-        def scale_columns_behind(n, k):
-            if n == POINTS - 1 and k == 0:
-                scale_quarter(n, 1, nc.vector, 0)
-
-        def scale_columns(n, k):
-            if k == 0 or n < POINTS - 1:
-                scale_quarter(n, k, nc.gpsimd, k)
-
-        def scale_quarter(n, j, engine, release):
+        def scale_columns(n, j, engine, inverse):
             if n not in attn_grouped:
-                attn_grouped[n] = attn_pool.tile([P, ENTRIES, PACK], BF16, name="attn_grouped", align_bytes=64)
+                attn_grouped[n] = grouped_pool.tile([P, ENTRIES, PACK], BF16, name="attn_grouped", align_bytes=64)
                 attn_codes[n] = mx_pool.tile([P, ENTRIES], U32, name="attn_codes", align_bytes=64)
                 attn_scales[n] = mx_pool.tile([P, ENTRIES], U8, name="attn_scales", align_bytes=64)
             queries = slice(j * P, (j + 1) * P)
             engine.tensor_tensor(
-                out=attn_grouped[n][:, queries, :].rearrange("p (b i) t -> p b t i", i=4),
-                in0=prob_t[n][:, :, queries].rearrange("p t (b i) -> p b t i", i=4),
-                in1=inv[PACK * n + release + COL - 1][:, 0:PACK].unsqueeze(1).unsqueeze(3).to_broadcast([P, P // 4, PACK, 4]),
+                out=attn_grouped[n][:, queries, :].rearrange("p (b i) t -> p b t i", i=RUN),
+                in0=prob_t[n][:, :, queries].rearrange("p t (b i) -> p b t i", i=RUN),
+                in1=inverse[:, 0:PACK].unsqueeze(1).unsqueeze(3).to_broadcast([P, P // RUN, PACK, RUN]),
                 op=ALU.mult,
             )
 
-        def quantise_attention(n, j):
-            if j == 0:
-                quantise(attn_codes[n], attn_scales[n], attn_grouped[n], 0, ENTRIES)
+        def scale_columns_on_gpsimd(n, j):
+            if n < LAST or j == 0:
+                scale_columns(n, j, nc.gpsimd, inverses[PACK * n + j + COLUMNS_DELAY - 1])
 
-        def output_mx(n, j):
-            queries = slice(j * P, (j + 1) * P)
-            if n == POINTS - 1 and j % 2 == 1:
-                yr_acc[n, j] = psum_energy.tile([P, CHANNELS], F32, name="energy")
+        def scale_columns_on_vector(n, j):
+            if n == LAST and j == 0:
+                scale_columns(n, 1, nc.vector, inverses[PACK * n + COLUMNS_DELAY - 1])
+            elif n == LAST and j == 1:
+                scale_columns(n, 2, nc.vector, inverses[PACK * n + COLUMNS_DELAY - 1])
+                scale_columns(n, 3, nc.vector, inverses[PACK * n + COLUMNS_DELAY - 1])
+
+        def quantise_attention(n, j):
+            early = (LAST - 2, LAST)
+            if j == PACK - 1 and n + 1 in early:
+                quantise(attn_codes[n + 1], attn_scales[n + 1], attn_grouped[n + 1])
+            if j == 0 and n not in early:
+                quantise(attn_codes[n], attn_scales[n], attn_grouped[n])
+
+        def attend(n, j):
+            if n >= LAST - 1 and j % 2 == 1:
+                yr_acc[n, j] = psum_energy.tile([P, CHANNELS], F32, name="late_output", tag="energy")
             else:
                 yr_acc[n, j] = psum_mx.tile([P, CHANNELS], F32, name="yr_acc", tag="acc")
+            queries = slice(j * P, (j + 1) * P)
             nc.tensor.matmul_mx(
                 out=yr_acc[n, j][:],
                 lhsT=attn_codes[n][:, queries].bitcast(FP8X4),
@@ -390,59 +334,50 @@ def tile_interral_pa_kernel(tc, xq, yk, y_feat, x_feat, W_v, b_v, out):
 
         def subtract_attended(n, j):
             result = result_pool.tile([P, CHANNELS], F32)
-            if (n, j) in SUBG or j in SUBG:
-                staged = result_pool.tile([P, CHANNELS], F32, name="staged", bufs=2)
-                nc.scalar.copy(out=staged[:], in_=yr_acc[n, j][:])
-                nc.gpsimd.tensor_tensor(out=result[:], in0=x_sb[n][:, j, :], in1=staged[:], op=ALU.subtract)
-            else:
-                nc.vector.tensor_tensor(out=result[:], in0=x_sb[n][:, j, :], in1=yr_acc[n, j][:], op=ALU.subtract)
+            nc.vector.tensor_tensor(out=result[:], in0=x_sb[n][:, j, :], in1=yr_acc[n, j][:], op=ALU.subtract)
             nc.sync.dma_start(out=out_rows[n, j], in_=result[:])
 
-        ROW = {0: "D", 1: "S", 2: "S", 3: "S"}
-        SUBG = ()
-
-        def run(stage, index, count=QUARTERS):
-            if 0 <= index < count:
+        def run(stage, index):
+            if 0 <= index < QUARTERS:
                 stage(index // PACK, index % PACK)
 
-        def run_pairs(stage, index):
+        def run_groups(stage, index):
             if 0 <= index < QUARTERS and index % PACK < 2:
-                for t in (2 * (index % PACK), 2 * (index % PACK) + 1):
-                    stage(index // PACK, t)
+                stage(index // PACK, 2 * (index % PACK))
+                stage(index // PACK, 2 * (index % PACK) + 1)
 
-        w_grouped = resident.tile([P, CHANNELS, PACK], BF16, align_bytes=64)
-        w_codes = resident.tile([P, CHANNELS], U32, align_bytes=64)
-        w_scales = resident.tile([P, CHANNELS], U8, align_bytes=64)
+        def run_weights(stage, index):
+            if 0 <= index < PACK:
+                stage(index)
 
         with tc.manual_schedule():
-            for tick in range(-PROJ_LEAD - 1, QUARTERS + OUT):
-                run(row_max, tick)
-                run(evacuate_projections, tick + PROJ_LEAD)
-                run(add_epsilon, tick - COL)
-                run(quantise_weights, tick + WL - 2, PACK)
-                run(quantise_features, tick - 4)
-                run(quantise_attention, tick - AQ)
-                run(scale_columns_on_vector, tick - COL)
-                run(invert, tick - 1, QUARTERS + 4 * PACK)
-                run(scale_columns_behind, tick - COL)
-                run(quantise_values, tick - VQ)
-                run(add_bias_turned, tick - VALUES)
-                run(build_diagonal, tick - 2)
-                run(scale_rows, tick - 2)
-                run_pairs(sum_columns, tick - FLIP)
-                run(exponentials, tick)
-                run(scale_columns, tick - COL)
-                run(evacuate_weights, tick + WL, PACK)
-                run(evacuate_features, tick + FEAT_LEAD)
-                run(add_bias, tick - VALUES)
-                run(subtract_attended, tick - OUT)
-                if tick != 0:
-                    run(energies, tick + 1)
+            for tick in range(-PROJECTIONS_LEAD - 1, QUARTERS + OUTPUT_DELAY):
+                run(find_row_max, tick)
+                run(evacuate_projections, tick + PROJECTIONS_LEAD)
+                run(add_epsilon, tick - COLUMNS_DELAY)
+                run_weights(quantise_weights, tick - WEIGHTS_QUANTISE_DELAY)
+                run(quantise_features, tick - FEATURES_QUANTISE_DELAY)
+                run(quantise_attention, tick - ATTENTION_QUANTISE_DELAY)
+                if 0 <= tick - 1 < QUARTERS + COLUMNS_DELAY - PACK + 1:
+                    invert_sums(tick - 1)
+                run(scale_columns_on_vector, tick - COLUMNS_DELAY)
+                run(quantise_values, tick - VALUES_QUANTISE_DELAY)
+                run(scale_rows, tick - ROWS_DELAY)
+                run_groups(sum_columns, tick - TURN_DELAY)
+                run(exponentiate, tick)
+                run(scale_columns_on_gpsimd, tick - COLUMNS_DELAY)
+                run_weights(evacuate_weights, tick - WEIGHTS_DELAY)
+                run(evacuate_features, tick)
+                run(add_bias, tick - VALUES_DELAY)
+                run(subtract_attended, tick - OUTPUT_DELAY)
                 if tick == -1:
-                    run(energies, 1)
-                run(prepare_projections, tick + PROJ_LEAD + 1)
-                run(prepare_weights, tick + WL + 1, PACK)
-                run(prepare_features, tick + FEAT_LEAD + 1)
-                run_pairs(flip_probabilities, tick + 1 - FLIP)
-                run(values_mx, tick + 1 - VALUES)
-                run(output_mx, tick + 1 - OUT)
+                    multiply_energies(0, 0)
+                    multiply_energies(0, 1)
+                elif tick > 0:
+                    run(multiply_energies, tick + 1)
+                run(turn_projections, tick + 1 + PROJECTIONS_LEAD)
+                run_weights(turn_weights, tick + 1 - WEIGHTS_DELAY)
+                run(turn_features, tick + 1)
+                run_groups(turn_probabilities, tick + 1 - TURN_DELAY)
+                run(project_values, tick + 1 - VALUES_DELAY)
+                run(attend, tick + 1 - OUTPUT_DELAY)

from contextlib import ExitStack

import concourse.mybir as mybir
from concourse.masks import make_identity

F32 = mybir.dt.float32
BF16 = mybir.dt.bfloat16
U32 = mybir.dt.uint32
U8 = mybir.dt.uint8
FP8X4 = mybir.dt.float8_e4m3fn_x4
ALU = mybir.AluOpType
ACT = mybir.ActivationFunctionType

P = 128
PACK = 4
POINTS = 8
LAST = POINTS - 1
ENTRIES = 512
CHANNELS = 512
QK = 128
EPS_L1 = 1e-9
RUN = 4

FLOPS = 2 * POINTS * ENTRIES * (CHANNELS * CHANNELS + ENTRIES * QK + ENTRIES * CHANNELS)

QUARTERS = POINTS * PACK
PROJECTIONS_LEAD = 4
WEIGHTS_DELAY = 1
WEIGHTS_QUANTISE_DELAY = 3
FEATURES_QUANTISE_DELAY = 4
VALUES_DELAY = 5
ROWS_DELAY = 2
TURN_DELAY = 6
COLUMNS_DELAY = 8
VALUES_QUANTISE_DELAY = 11
ATTENTION_QUANTISE_DELAY = 13
OUTPUT_DELAY = 14

DIAGONAL_QUARTER = 0
KEYS_ON_VECTOR = (0, 1, 2)
FEATURES_ON_VECTOR = (1, 2)


def tile_interral_pa_kernel(tc, xq, yk, y_feat, x_feat, W_v, b_v, out):
    nc = tc.nc
    with ExitStack() as ctx:
        resident = ctx.enter_context(tc.tile_pool(name="resident", bufs=1))
        proj = ctx.enter_context(tc.tile_pool(name="proj", bufs=3))
        grouped_pool = ctx.enter_context(tc.tile_pool(name="grouped", bufs=2))
        mx_pool = ctx.enter_context(tc.tile_pool(name="mx", bufs=2))
        values_pool = ctx.enter_context(tc.tile_pool(name="values", bufs=5))
        soft = ctx.enter_context(tc.tile_pool(name="soft", bufs=3))
        stats = ctx.enter_context(tc.tile_pool(name="stats", bufs=4))
        inverse_pool = ctx.enter_context(tc.tile_pool(name="inverse", bufs=8))
        diagonal_pool = ctx.enter_context(tc.tile_pool(name="diagonal", bufs=6))
        result_pool = ctx.enter_context(tc.tile_pool(name="result", bufs=8))
        psum_turn = ctx.enter_context(tc.psum_pool(name="psum_turn", bufs=4))
        psum_energy = ctx.enter_context(tc.psum_pool(name="psum_energy", bufs=2))
        psum_mx = ctx.enter_context(tc.psum_pool(name="psum_mx", bufs=2))

        xq_rows = xq.rearrange("n (p g) d -> n p g d", g=PACK)
        yk_rows = yk.rearrange("n (p g) d -> n p g d", g=PACK)
        y_rows = y_feat.rearrange("(p g) n k -> n p g k", g=PACK)
        x_rows = x_feat.rearrange("(p g) n c -> n p g c", g=PACK)
        out_rows = out.rearrange("(p g) n c -> n g p c", g=PACK)

        xq_sb, yk_sb, y_sb, x_sb = [], [], [], []
        w_sb = resident.tile([P, PACK, CHANNELS], BF16)
        bias_sb = resident.tile([P, CHANNELS], BF16)
        for n in range(POINTS):
            xq_sb.append(resident.tile([P, PACK, QK], BF16, name="xq%d" % n))
            yk_sb.append(resident.tile([P, PACK, QK], BF16, name="yk%d" % n))
            y_sb.append(resident.tile([P, PACK, CHANNELS], BF16, name="y%d" % n))
            x_sb.append(resident.tile([P, PACK, CHANNELS], BF16, name="x%d" % n))

        def load_projections(n):
            nc.sync.dma_start(out=xq_sb[n][:], in_=xq_rows[n])
            nc.sync.dma_start(out=yk_sb[n][:], in_=yk_rows[n])

        load_projections(0)
        load_projections(1)
        for n in range(POINTS):
            if 0 < n < LAST:
                load_projections(n + 1)
            nc.sync.dma_start(out=y_sb[n][:], in_=y_rows[n])
            if n == 0:
                nc.sync.dma_start(out=w_sb[:], in_=W_v.rearrange("(i p) k -> p i k", p=P))
                nc.sync.dma_start(out=bias_sb[:], in_=b_v.partition_broadcast(P))
            elif n > 1:
                nc.sync.dma_start(out=x_sb[n - 2][:], in_=x_rows[n - 2])
        for n in (LAST - 1, LAST):
            nc.sync.dma_start(out=x_sb[n][:], in_=x_rows[n])

        ident_f32 = resident.tile([P, P], F32)
        make_identity(nc, ident_f32[:])
        ident_bf16 = resident.tile([P, P], BF16)
        make_identity(nc, ident_bf16[:])

        w_grouped = resident.tile([P, CHANNELS, PACK], BF16, align_bytes=64)
        w_codes = resident.tile([P, CHANNELS], U32, align_bytes=64)
        w_scales = resident.tile([P, CHANNELS], U8, align_bytes=64)

        turned_w, turned_y, turned_proj, turned_p = {}, {}, {}, {}
        y_grouped, y_codes, y_scales = {}, {}, {}
        xq_t, yk_t = {}, {}
        energy, neg_max, prob = {}, {}, {}
        sums, inverses, diagonal = {}, {}, {}
        yv_acc, yv_grouped, yv_codes, yv_scales = {}, {}, {}, {}
        col_sum, prob_t = {}, {}
        attn_grouped, attn_codes, attn_scales, yr_acc = {}, {}, {}, {}

        def quantise(codes, scales, grouped):
            nc.vector.quantize_mx(
                out=codes[:].bitcast(FP8X4), scales=scales[:], in_=grouped[:].rearrange("q r t -> q (r t)")
            )

        def turn_channels(rows_sb, pair):
            words = rows_sb[:].bitcast(F32)
            turned = psum_turn.tile([P, 2, 2, P], F32, name="turned_channels", tag="turn")
            for g in range(2):
                for u in range(2):
                    nc.tensor.transpose(
                        turned[:, g, u, :], words[:, 2 * pair + g, u * P : (u + 1) * P], ident_f32[:]
                    )
            return turned

        def evacuate_channels(turned, grouped, pair, copy):
            words = grouped[:].bitcast(F32).rearrange("q (g r) u -> q g r u", g=PACK)
            copy(out=words[:, 2 * pair : 2 * pair + 2], in_=turned[:].rearrange("q g u r -> q g r u"))

        def turn_weights(j):
            if j < 2:
                turned_w[j] = turn_channels(w_sb, j)

        def evacuate_weights(j):
            if j < 2:
                evacuate_channels(turned_w[j], w_grouped, j, nc.vector.tensor_copy)

        def quantise_weights(j):
            if j == 0:
                quantise(w_codes, w_scales, w_grouped)

        def turn_features(n, j):
            if j < 2:
                turned_y[n, j] = turn_channels(y_sb[n], j)

        def evacuate_features(n, j):
            if j == 0:
                y_grouped[n] = grouped_pool.tile([P, ENTRIES, PACK], BF16, name="y_grouped", align_bytes=64)
                y_codes[n] = mx_pool.tile([P, ENTRIES], U32, name="y_codes", align_bytes=64)
                y_scales[n] = mx_pool.tile([P, ENTRIES], U8, name="y_scales", align_bytes=64)
            if j < 2:
                copy = nc.vector.tensor_copy if n in FEATURES_ON_VECTOR else nc.scalar.copy
                evacuate_channels(turned_y[n, j], y_grouped[n], j, copy)

        def quantise_features(n, j):
            if j == 0:
                quantise(y_codes[n], y_scales[n], y_grouped[n])

        def turn_projections(n, j):
            if j < 2:
                rows_sb = (xq_sb, yk_sb)[j][n]
                turned_proj[n, j] = psum_turn.tile([P, PACK, P], BF16, name="turned_proj", tag="turn")
                for g in range(PACK):
                    nc.tensor.transpose(turned_proj[n, j][:, g, :], rows_sb[:, g, :], ident_bf16[:])

        def evacuate_projections(n, j):
            if j < 2:
                copy = nc.vector.tensor_copy if j == 1 and n in KEYS_ON_VECTOR else nc.scalar.copy
                columns = proj.tile([P, ENTRIES], BF16, name=("xq_t", "yk_t")[j])
                (xq_t, yk_t)[j][n] = columns
                copy(out=columns[:], in_=turned_proj[n, j][:].rearrange("d g r -> d (g r)"))

        def project_values(n, c):
            if c == 0:
                yv_grouped[n] = grouped_pool.tile([P, CHANNELS, PACK], BF16, name="yv_grouped", align_bytes=64)
                yv_codes[n] = values_pool.tile([P, CHANNELS], U32, name="yv_codes", align_bytes=64)
                yv_scales[n] = values_pool.tile([P, CHANNELS], U8, name="yv_scales", align_bytes=64)
            if n == LAST:
                yv_acc[n, c] = psum_energy.tile([P, PACK, P], F32, name="late_values", tag="energy")
            else:
                yv_acc[n, c] = psum_mx.tile([P, PACK, P], F32, name="yv_acc", tag="acc")
            cols = slice(c * P, (c + 1) * P)
            for t in range(PACK):
                keys = slice(t * P, (t + 1) * P)
                nc.tensor.matmul_mx(
                    out=yv_acc[n, c][:, t, :],
                    lhsT=y_codes[n][:, keys].bitcast(FP8X4),
                    lhsT_scale=y_scales[n][:, keys],
                    rhs=w_codes[:, cols].bitcast(FP8X4),
                    rhs_scale=w_scales[:, cols],
                    start=True,
                    stop=True,
                )

        def add_bias(n, c):
            cols = slice(c * P, (c + 1) * P)
            nc.vector.tensor_tensor(
                out=yv_grouped[n][:, cols, :],
                in0=yv_acc[n, c][:].rearrange("p t c -> p c t"),
                in1=bias_sb[:, cols].unsqueeze(2).to_broadcast([P, P, PACK]),
                op=ALU.add,
            )

        def quantise_values(n, j):
            if j == 0:
                quantise(yv_codes[n], yv_scales[n], yv_grouped[n])

        def multiply_energies(n, j):
            if n == 0 and j > 1:
                energy[n, j] = psum_mx.tile([P, ENTRIES], F32, name="early_energy", tag="acc")
            else:
                energy[n, j] = psum_energy.tile([P, ENTRIES], F32, name="energy", tag="energy")
            nc.tensor.matmul(
                out=energy[n, j][:], lhsT=xq_t[n][:, j * P : (j + 1) * P], rhs=yk_t[n][:], start=True, stop=True
            )

        def find_row_max(n, j):
            if j == 0:
                neg_max[n] = stats.tile([P, PACK], F32, name="neg_max")
                prob[n] = soft.tile([P, PACK, ENTRIES], F32, name="prob")
            nc.vector.tensor_reduce(
                out=neg_max[n][:, j : j + 1], in_=energy[n, j][:], axis=mybir.AxisListType.X, op=ALU.max, negate=True
            )

        def sums_of(index):
            shifted = index + (1 - COLUMNS_DELAY) % PACK
            if shifted // PACK not in sums:
                sums[shifted // PACK] = stats.tile([P, 2 * PACK], F32, name="sums")
            return sums[shifted // PACK], PACK + shifted % PACK

        def exponentiate(n, j):
            tile, column = sums_of(PACK * n + j)
            nc.scalar.activation(
                out=prob[n][:, j, :],
                in_=energy[n, j][:],
                func=ACT.Exp,
                bias=neg_max[n][:, j : j + 1],
                scale=1.0,
                accum_out=tile[:, column : column + 1],
            )

        def add_epsilon(n, j):
            if j == 0:
                tile = sums_of(PACK * n + COLUMNS_DELAY - 1)[0]
                nc.vector.tensor_scalar_add(out=tile[:, 0:PACK], in0=col_sum[n][:], scalar1=EPS_L1)

        def invert_sums(index):
            tile, column = sums_of(index)
            n, j = (index + 1 - COLUMNS_DELAY) // PACK, (index + 1 - COLUMNS_DELAY) % PACK
            has_columns = 0 <= n < POINTS
            first_row = PACK + (1 - COLUMNS_DELAY) % PACK if tile is sums_of(0)[0] else PACK
            first = 0 if has_columns else first_row
            last = column + 1 if index < QUARTERS else PACK
            if n == LAST and j > 0:
                return
            inverses[index] = inverse_pool.tile([P, 2 * PACK], F32, name="inverses")
            nc.vector.reciprocal(out=inverses[index][:, first:last], in_=tile[:, first:last])

        def scale_rows(n, j):
            index = PACK * n + j
            column = sums_of(index)[1]
            inverse = inverses[index][:, column : column + 1]
            if j == DIAGONAL_QUARTER:
                diagonal[n] = diagonal_pool.tile([P, P], F32, name="diagonal")
                nc.scalar.activation(out=diagonal[n][:], in_=ident_f32[:], func=ACT.Copy, scale=inverse)
            else:
                nc.scalar.activation(out=prob[n][:, j, :], in_=prob[n][:, j, :], func=ACT.Copy, scale=inverse)

        def turn_probabilities(n, t):
            if t == 0:
                col_sum[n] = stats.tile([P, PACK], F32, name="col_sum")
                prob_t[n] = soft.tile([P, PACK, ENTRIES], F32, name="prob_t")
            turned_p[n, t] = psum_turn.tile([P, ENTRIES], F32, name="turned_p", tag="turn")
            for j in range(PACK):
                target = turned_p[n, t][:, j * P : (j + 1) * P]
                source = prob[n][:, j, t * P : (t + 1) * P]
                if j == DIAGONAL_QUARTER:
                    nc.tensor.matmul(out=target, lhsT=source, rhs=diagonal[n][:], start=True, stop=True)
                else:
                    nc.tensor.transpose(target, source, ident_f32[:])

        def sum_columns(n, t):
            nc.scalar.activation(
                out=prob_t[n][:, t, :], in_=turned_p[n, t][:], func=ACT.Copy, accum_out=col_sum[n][:, t : t + 1]
            )

        def scale_columns(n, j, engine, inverse):
            if n not in attn_grouped:
                attn_grouped[n] = grouped_pool.tile([P, ENTRIES, PACK], BF16, name="attn_grouped", align_bytes=64)
                attn_codes[n] = mx_pool.tile([P, ENTRIES], U32, name="attn_codes", align_bytes=64)
                attn_scales[n] = mx_pool.tile([P, ENTRIES], U8, name="attn_scales", align_bytes=64)
            queries = slice(j * P, (j + 1) * P)
            engine.tensor_tensor(
                out=attn_grouped[n][:, queries, :].rearrange("p (b i) t -> p b t i", i=RUN),
                in0=prob_t[n][:, :, queries].rearrange("p t (b i) -> p b t i", i=RUN),
                in1=inverse[:, 0:PACK].unsqueeze(1).unsqueeze(3).to_broadcast([P, P // RUN, PACK, RUN]),
                op=ALU.mult,
            )

        def scale_columns_on_gpsimd(n, j):
            if n < LAST or j == 0:
                scale_columns(n, j, nc.gpsimd, inverses[PACK * n + j + COLUMNS_DELAY - 1])

        def scale_columns_on_vector(n, j):
            if n == LAST and j == 0:
                scale_columns(n, 1, nc.vector, inverses[PACK * n + COLUMNS_DELAY - 1])
            elif n == LAST and j == 1:
                scale_columns(n, 2, nc.vector, inverses[PACK * n + COLUMNS_DELAY - 1])
                scale_columns(n, 3, nc.vector, inverses[PACK * n + COLUMNS_DELAY - 1])

        def quantise_attention(n, j):
            early = (LAST - 2, LAST)
            if j == PACK - 1 and n + 1 in early:
                quantise(attn_codes[n + 1], attn_scales[n + 1], attn_grouped[n + 1])
            if j == 0 and n not in early:
                quantise(attn_codes[n], attn_scales[n], attn_grouped[n])

        def attend(n, j):
            if n >= LAST - 1 and j % 2 == 1:
                yr_acc[n, j] = psum_energy.tile([P, CHANNELS], F32, name="late_output", tag="energy")
            else:
                yr_acc[n, j] = psum_mx.tile([P, CHANNELS], F32, name="yr_acc", tag="acc")
            queries = slice(j * P, (j + 1) * P)
            nc.tensor.matmul_mx(
                out=yr_acc[n, j][:],
                lhsT=attn_codes[n][:, queries].bitcast(FP8X4),
                lhsT_scale=attn_scales[n][:, queries],
                rhs=yv_codes[n][:].bitcast(FP8X4),
                rhs_scale=yv_scales[n][:],
                start=True,
                stop=True,
            )

        def subtract_attended(n, j):
            result = result_pool.tile([P, CHANNELS], F32)
            nc.vector.tensor_tensor(out=result[:], in0=x_sb[n][:, j, :], in1=yr_acc[n, j][:], op=ALU.subtract)
            nc.sync.dma_start(out=out_rows[n, j], in_=result[:])

        def run(stage, index):
            if 0 <= index < QUARTERS:
                stage(index // PACK, index % PACK)

        def run_groups(stage, index):
            if 0 <= index < QUARTERS and index % PACK < 2:
                stage(index // PACK, 2 * (index % PACK))
                stage(index // PACK, 2 * (index % PACK) + 1)

        def run_weights(stage, index):
            if 0 <= index < PACK:
                stage(index)

        with tc.manual_schedule():
            for tick in range(-PROJECTIONS_LEAD - 1, QUARTERS + OUTPUT_DELAY):
                run(find_row_max, tick)
                run(evacuate_projections, tick + PROJECTIONS_LEAD)
                run(add_epsilon, tick - COLUMNS_DELAY)
                run_weights(quantise_weights, tick - WEIGHTS_QUANTISE_DELAY)
                run(quantise_features, tick - FEATURES_QUANTISE_DELAY)
                run(quantise_attention, tick - ATTENTION_QUANTISE_DELAY)
                if 0 <= tick - 1 < QUARTERS + COLUMNS_DELAY - PACK + 1:
                    invert_sums(tick - 1)
                run(scale_columns_on_vector, tick - COLUMNS_DELAY)
                run(quantise_values, tick - VALUES_QUANTISE_DELAY)
                run(scale_rows, tick - ROWS_DELAY)
                run_groups(sum_columns, tick - TURN_DELAY)
                run(exponentiate, tick)
                run(scale_columns_on_gpsimd, tick - COLUMNS_DELAY)
                run_weights(evacuate_weights, tick - WEIGHTS_DELAY)
                run(evacuate_features, tick)
                run(add_bias, tick - VALUES_DELAY)
                run(subtract_attended, tick - OUTPUT_DELAY)
                if tick == -1:
                    multiply_energies(0, 0)
                    multiply_energies(0, 1)
                elif tick > 0:
                    run(multiply_energies, tick + 1)
                run(turn_projections, tick + 1 + PROJECTIONS_LEAD)
                run_weights(turn_weights, tick + 1 - WEIGHTS_DELAY)
                run(turn_features, tick + 1)
                run_groups(turn_probabilities, tick + 1 - TURN_DELAY)
                run(project_values, tick + 1 - VALUES_DELAY)
                run(attend, tick + 1 - OUTPUT_DELAY)
